import numpy as np
import ml_dtypes


def mxq(x, axis, fmt="e4m3"):
    dtype, down = {"e4m3": (ml_dtypes.float8_e4m3fn, 7), "e5m2": (ml_dtypes.float8_e5m2, 14)}[fmt]
    v = np.moveaxis(np.asarray(x, np.float32).astype(ml_dtypes.bfloat16).astype(np.float64), axis, -1)
    blocks = v.reshape(v.shape[:-1] + (-1, 32))
    amax = np.abs(blocks).max(-1, keepdims=True)
    byte = np.maximum(np.where(amax > 0, np.frexp(amax)[1] - 1 + 127, 0) - down, 1)
    scale = np.exp2(byte - 127.0)
    codes = (blocks / scale).astype(np.float32).astype(dtype).astype(np.float64)
    return np.moveaxis((codes * scale).reshape(v.shape), -1, axis)


WIDE = False


def mx_kscale(k):
    if not WIDE:
        return np.ones(k)
    levels = np.array([10, -10, 5, -5, 0])
    if k % 512:
        return np.exp2(np.random.permutation(np.resize(levels, k // 32))).repeat(32)
    a = np.empty((k // 512, 16))
    for p in range(k // 512):
        a[p, :8] = np.random.permutation(np.resize(levels, 8))
        for g in range(8):
            far = levels[np.abs(levels - a[p, g]) >= 10]
            a[p, g + 8] = far[np.random.randint(len(far))]
    return np.exp2(a.ravel()).repeat(32)


BF16 = ml_dtypes.bfloat16


def bf(x):
    return np.asarray(x, np.float32).astype(BF16)


def f64(x):
    return np.asarray(x).astype(np.float64)


B, IN, H = 512, 1024, 1024


def sigmoid(v):
    return 1.0 / (1.0 + np.exp(-v))


def setup_inputs():
    s, t = mx_kscale(IN), mx_kscale(H)
    a = np.sqrt(2.0 / (IN + H))
    d = 0.3 + np.random.standard_normal((B, H)) * 1.6
    return {
        "x": bf(np.random.standard_normal((B, IN)) * s),
        "h_prev": bf(np.random.standard_normal((B, H)) * t),
        "c_prev": bf(np.random.standard_normal((B, H))),
        "n_prev": bf(1.0 + np.random.standard_normal((B, H)) * 0.1),
        "i_prime": bf(np.exp(np.minimum(d, 0.0))),
        "f_prime": bf(np.exp(np.minimum(-d, 0.0))),
        "Wz_x": bf(np.random.standard_normal((H, IN)) * a / s),
        "b_z": bf(np.random.standard_normal(H) * 0.3),
        "Wz_h": bf(np.random.standard_normal((H, H)) * a / t),
        "Wo_x": bf(np.random.standard_normal((H, IN)) * a / s),
        "b_o": bf(np.random.standard_normal(H) * 0.3),
        "Wo_h": bf(np.random.standard_normal((H, H)) * a / t),
    }


def reference(x, h_prev, c_prev, n_prev, i_prime, f_prime, Wz_x, b_z, Wz_h, Wo_x, b_o, Wo_h):
    xq = mxq(f64(x), 1, "e4m3")
    hq = mxq(f64(h_prev), 1, "e4m3")
    z_aff = (xq @ mxq(f64(Wz_x), 1, "e4m3").T) + f64(b_z) + (hq @ mxq(f64(Wz_h), 1, "e4m3").T)
    o_aff = (xq @ mxq(f64(Wo_x), 1, "e4m3").T) + f64(b_o) + (hq @ mxq(f64(Wo_h), 1, "e4m3").T)
    z = np.tanh(z_aff)
    c_t = f64(f_prime) * f64(c_prev) + f64(i_prime) * z
    n_t = f64(f_prime) * f64(n_prev) + f64(i_prime)
    h_t = sigmoid(o_aff) * (c_t / np.maximum(n_t, 1e-6))
    return h_t, c_t

@@ -1,0 +1,266 @@
+from contextlib import ExitStack
+
+import concourse.mybir as mybir
+from concourse.masks import make_identity
+
+F32 = mybir.dt.float32
+BF16 = mybir.dt.bfloat16
+U32 = mybir.dt.uint32
+U8 = mybir.dt.uint8
+FP8X4 = mybir.dt.float8_e4m3fn_x4
+ACT = mybir.ActivationFunctionType
+ALU = mybir.AluOpType
+
+P = 128
+PACK = 4
+BATCH = 512
+FEATURES = 1024
+BATCH_TILES = BATCH // P
+FEATURE_TILES = FEATURES // P
+SOURCES = 2
+SOURCE_PASSES = FEATURES // (P * PACK)
+PASSES = SOURCES * SOURCE_PASSES
+WORDS = FEATURES // 2
+WORD_BLOCKS = WORDS // P
+GATES = 2
+N_FLOOR = 1e-6
+
+FLOPS = 2 * BATCH * (SOURCES * FEATURES) * (GATES * FEATURES)
+
+
+def tile_slstmlayer_pb_kernel(
+    tc, x, h_prev, c_prev, n_prev, i_prime, f_prime, Wz_x, b_z, Wz_h, Wo_x, b_o, Wo_h, out_0, out_1
+):
+    nc = tc.nc
+    gate_function = (ACT.Tanh, ACT.Sigmoid)
+
+    def by_batch_tile(dram):
+        return dram.rearrange("(p t) f -> p t f", t=BATCH_TILES)
+
+    with ExitStack() as ctx:
+        ctx.enter_context(tc.manual_schedule())
+        keep = ctx.enter_context(tc.tile_pool(name="keep", bufs=1))
+        regrouped = ctx.enter_context(tc.tile_pool(name="regrouped", bufs=4))
+        quantised = ctx.enter_context(tc.tile_pool(name="quantised", bufs=4))
+        work = ctx.enter_context(tc.tile_pool(name="work", bufs=2))
+        flipped_banks = ctx.enter_context(tc.psum_pool(name="flipped_banks", bufs=4))
+        product_banks = ctx.enter_context(tc.psum_pool(name="product_banks", bufs=2))
+        gate_banks = ctx.enter_context(tc.psum_pool(name="gate_banks", bufs=2))
+
+        identity = keep.tile([P, P], F32, name="identity")
+        act_raw = [keep.tile([P, BATCH_TILES * FEATURES], BF16, name="act_raw%d" % s) for s in range(SOURCES)]
+        w_raw = [
+            [keep.tile([P, FEATURE_TILES * FEATURES], BF16, name="w_raw%d%d" % (gate, s)) for s in range(SOURCES)]
+            for gate in range(GATES)
+        ]
+        f_sb = keep.tile([P, BATCH_TILES, FEATURES], BF16, name="f_sb")
+        n_sb = keep.tile([P, BATCH_TILES, FEATURES], BF16, name="n_sb")
+        i_sb = keep.tile([P, BATCH_TILES, FEATURES], BF16, name="i_sb")
+        c_sb = keep.tile([P, BATCH_TILES, FEATURES], BF16, name="c_sb")
+        cell = keep.tile([P, BATCH_TILES, FEATURES], F32, name="cell")
+        readout = keep.tile([P, BATCH_TILES, FEATURES], F32, name="readout")
+        act_grouped = [
+            keep.tile([P, SOURCE_PASSES * BATCH * PACK], BF16, name="act_grouped%d" % s, align_bytes=64)
+            for s in range(SOURCES)
+        ]
+        act_codes = keep.tile([P, PASSES, BATCH], U32, name="act_codes", align_bytes=64)
+        act_scales = keep.tile([P, PASSES, BATCH], U8, name="act_scales", align_bytes=64)
+
+        ones = keep.tile([P, 1], F32, name="ones")
+        warm = keep.tile([P, 1], F32, name="warm")
+        nc.vector.memset(ones[:], 1.0)
+        nc.scalar.activation(out=warm[:], in_=ones[:], func=ACT.Abs_reciprocal_sqrt)
+        make_identity(nc, identity[:])
+        bias_rows = keep.tile([P, P], BF16, name="bias_rows")
+        nc.vector.memset(bias_rows[:], 0.0)
+        for gate, bias in enumerate((b_z, b_o)):
+            nc.scalar.dma_start(
+                out=bias_rows[gate * FEATURE_TILES : (gate + 1) * FEATURE_TILES, :],
+                in_=bias.rearrange("(r c) -> r c", c=P),
+            )
+
+        def load_weights(ft):
+            for gate, pair in enumerate(((Wz_x, Wz_h), (Wo_x, Wo_h))):
+                for s, dram in enumerate(pair):
+                    nc.sync.dma_start(
+                        out=w_raw[gate][s][:, ft * FEATURES : (ft + 1) * FEATURES],
+                        in_=dram[ft * P : (ft + 1) * P, :],
+                    )
+
+        def load_gates(tiles):
+            for t in tiles:
+                for sbuf, dram in ((f_sb, f_prime), (n_sb, n_prev)):
+                    nc.sync.dma_start(out=sbuf[:, t, :], in_=by_batch_tile(dram)[:, t, :])
+            for t in tiles:
+                nc.sync.dma_start(out=i_sb[:, t, :], in_=by_batch_tile(i_prime)[:, t, :])
+
+        def load_activations(s, dram):
+            nc.sync.dma_start(out=act_raw[s][:].rearrange("p (t f) -> p t f", t=BATCH_TILES), in_=by_batch_tile(dram))
+
+        load_gates(range(0, BATCH_TILES // 2))
+        load_activations(0, x)
+        load_gates(range(BATCH_TILES // 2, BATCH_TILES))
+        load_weights(0)
+        load_activations(1, h_prev)
+        load_weights(1)
+        load_weights(2)
+        nc.sync.dma_start(out=c_sb[:], in_=by_batch_tile(c_prev))
+        for ft in range(3, FEATURE_TILES):
+            load_weights(ft)
+
+        def regroup_rows(words, grouped_words, on_vector=False):
+            bank = flipped_banks.tile([P, WORD_BLOCKS, P], F32, name="flipped")
+            for j in range(WORD_BLOCKS):
+                g, u = divmod(j, 2)
+                nc.tensor.transpose(bank[:, j, :], words[:, 2 * P * g + u : 2 * P * (g + 1) : 2], identity[:])
+            if on_vector:
+                nc.vector.tensor_copy(out=grouped_words, in_=bank[:].rearrange("q (g u) r -> q g r u", u=2))
+            else:
+                nc.scalar.copy(out=grouped_words, in_=bank[:].rearrange("q (g u) r -> q g r u", u=2))
+
+        def normaliser(tiles):
+            for t in tiles:
+                nc.vector.tensor_tensor(out=readout[:, t, :], in0=f_sb[:, t, :], in1=n_sb[:, t, :], op=ALU.mult)
+            for t in tiles:
+                nc.vector.tensor_tensor(out=readout[:, t, :], in0=readout[:, t, :], in1=i_sb[:, t, :], op=ALU.add)
+            for t in tiles:
+                nc.vector.tensor_scalar_max(out=readout[:, t, :], in0=readout[:, t, :], scalar1=N_FLOOR)
+
+        def reciprocal_root(tiles):
+            for t in tiles:
+                nc.scalar.activation(out=readout[:, t, :], in_=readout[:, t, :], func=ACT.Abs_reciprocal_sqrt)
+
+        def quantise_activations(s):
+            for g in range(SOURCE_PASSES):
+                nc.vector.quantize_mx(
+                    out=act_codes[:, s * SOURCE_PASSES + g, :].bitcast(FP8X4),
+                    scales=act_scales[:, s * SOURCE_PASSES + g, :],
+                    in_=act_grouped[s][:, g * BATCH * PACK : (g + 1) * BATCH * PACK],
+                )
+
+        w_grouped = {}
+        w_codes = {}
+        w_scales = {}
+        gate_rows = {}
+        gate_cols = {}
+
+        def transpose_weights(ft, gate):
+            grouped = regrouped.tile([P, PASSES * P * PACK], BF16, name="w_grouped", align_bytes=64)
+            grouped_words = grouped[:].bitcast(F32).rearrange("q (s g r u) -> q s g r u", s=SOURCES, g=SOURCE_PASSES, u=2)
+            for s in range(SOURCES):
+                words = w_raw[gate][s][:].bitcast(F32)[:, ft * WORDS : (ft + 1) * WORDS]
+                regroup_rows(words, grouped_words[:, s])
+            w_grouped[(ft, gate)] = grouped
+
+        def quantise_weights(ft, gate):
+            codes = quantised.tile([P, PASSES * P], U32, name="w_codes", align_bytes=64)
+            scales = quantised.tile([P, PASSES * P], U8, name="w_scales", align_bytes=64)
+            nc.vector.quantize_mx(out=codes[:].bitcast(FP8X4), scales=scales[:], in_=w_grouped[(ft, gate)][:])
+            w_codes[(ft, gate)] = codes
+            w_scales[(ft, gate)] = scales
+
+        def multiply_and_activate(ft, gate):
+            product = product_banks.tile([P, BATCH], F32, name="product")
+            for k in range(PASSES):
+                columns = slice(k * P, (k + 1) * P)
+                nc.tensor.matmul_mx(
+                    out=product[:],
+                    lhsT=w_codes[(ft, gate)][:, columns].bitcast(FP8X4),
+                    lhsT_scale=w_scales[(ft, gate)][:, columns],
+                    rhs=act_codes[:, k, :].bitcast(FP8X4),
+                    rhs_scale=act_scales[:, k, :],
+                    start=(k == 0),
+                    stop=(k == PASSES - 1),
+                )
+            rows = work.tile([P, BATCH], F32, name="gate_rows")
+            column = gate * FEATURE_TILES + ft
+            nc.scalar.activation(
+                out=rows[:], in_=product[:], func=gate_function[gate], bias=bias_cols[:, column : column + 1]
+            )
+            gate_rows[(ft, gate)] = rows
+
+        def transpose_back(ft, gate):
+            bank = gate_banks.tile([P, BATCH_TILES, P], F32, name="gate_cols")
+            for t in range(BATCH_TILES):
+                nc.tensor.transpose(bank[:, t, :], gate_rows[(ft, gate)][:, t * P : (t + 1) * P], identity[:])
+            gate_cols[(ft, gate)] = bank
+
+        kept_terms = {}
+
+        def prepare_states(ft):
+            cols = slice(ft * P, (ft + 1) * P)
+            nc.scalar.activation(out=readout[:, :, cols], in_=readout[:, :, cols], func=ACT.Square)
+            kept = work.tile([P, BATCH_TILES, P], F32, name="kept_term")
+            nc.gpsimd.tensor_tensor(out=kept[:], in0=f_sb[:, :, cols], in1=c_sb[:, :, cols], op=ALU.mult)
+            kept_terms[ft] = kept
+
+        input_terms = {}
+
+        def gate_products(ft):
+            cols = slice(ft * P, (ft + 1) * P)
+            input_term = work.tile([P, BATCH_TILES, P], F32, name="input_term")
+            nc.vector.tensor_tensor(out=input_term[:], in0=gate_cols[(ft, 0)][:], in1=i_sb[:, :, cols], op=ALU.mult)
+            nc.vector.tensor_tensor(out=readout[:, :, cols], in0=gate_cols[(ft, 1)][:], in1=readout[:, :, cols], op=ALU.mult)
+            input_terms[ft] = input_term
+
+        def finish_cell(ft):
+            cols = slice(ft * P, (ft + 1) * P)
+            nc.vector.tensor_tensor(out=cell[:, :, cols], in0=input_terms[ft][:], in1=kept_terms[ft][:], op=ALU.add)
+            nc.sync.dma_start(out=by_batch_tile(out_1)[:, :, cols], in_=cell[:, :, cols])
+
+        def finish_readout(ft):
+            cols = slice(ft * P, (ft + 1) * P)
+            nc.vector.tensor_tensor(out=readout[:, :, cols], in0=readout[:, :, cols], in1=cell[:, :, cols], op=ALU.mult)
+            nc.sync.dma_start(out=by_batch_tile(out_0)[:, :, cols], in_=readout[:, :, cols])
+
+        def regroup_activations(s):
+            words = act_raw[s][:].bitcast(F32).rearrange("p (t w) -> p t w", t=BATCH_TILES)
+            grouped_words = act_grouped[s][:].bitcast(F32).rearrange(
+                "q (g t r u) -> q g t r u", g=SOURCE_PASSES, t=BATCH_TILES, u=2
+            )
+            for t in range(BATCH_TILES):
+                regroup_rows(words[:, t, :], grouped_words[:, :, t], on_vector=(s == SOURCES - 1 and t % 2 == 1))
+
+        normaliser(range(0, BATCH_TILES // 2))
+        regroup_activations(0)
+        reciprocal_root(range(0, BATCH_TILES // 2))
+        bias_rows_f32 = keep.tile([P, P], F32, name="bias_rows_f32")
+        nc.vector.tensor_copy(out=bias_rows_f32[:], in_=bias_rows[:])
+        bias_bank = flipped_banks.tile([P, WORD_BLOCKS, P], F32, name="flipped")
+        nc.tensor.transpose(bias_bank[:, 0, :], bias_rows_f32[:], identity[:])
+        bias_cols = keep.tile([P, GATES * FEATURE_TILES], F32, name="bias_cols")
+        nc.vector.tensor_copy(out=bias_cols[:], in_=bias_bank[:, 0, 0 : GATES * FEATURE_TILES])
+        normaliser(range(BATCH_TILES // 2, BATCH_TILES))
+        quantise_activations(0)
+        for gate in range(GATES):
+            transpose_weights(0, gate)
+        reciprocal_root(range(BATCH_TILES // 2, BATCH_TILES))
+        for gate in range(GATES):
+            quantise_weights(0, gate)
+        regroup_activations(1)
+        quantise_activations(1)
+        prepare_states(0)
+
+        for ft in range(0, FEATURE_TILES + 1):
+            ahead = ft + 1
+            behind = ft - 1
+            if ahead < FEATURE_TILES:
+                for gate in range(GATES):
+                    transpose_weights(ahead, gate)
+            if behind >= 0:
+                for gate in range(GATES):
+                    transpose_back(behind, gate)
+            if ahead < FEATURE_TILES:
+                quantise_weights(ahead, 0)
+            if behind >= 0:
+                gate_products(behind)
+                finish_cell(behind)
+            if ahead < FEATURE_TILES:
+                quantise_weights(ahead, 1)
+            if behind >= 0:
+                finish_readout(behind)
+            if 0 <= ft < FEATURE_TILES:
+                for gate in range(GATES):
+                    multiply_and_activate(ft, gate)
+            if ahead < FEATURE_TILES:
+                prepare_states(ahead)

@@ -235,6 +235,7 @@ def tile_slstmlayer_pb_kernel(
         for gate in range(GATES):
             transpose_weights(0, gate)
         reciprocal_root(range(BATCH_TILES // 2, BATCH_TILES))
+        nc.scalar.activation(out=warm[:], in_=ones[:], func=ACT.Sigmoid)
         for gate in range(GATES):
             quantise_weights(0, gate)
         regroup_activations(1)

@@ -196,12 +196,15 @@ def tile_slstmlayer_pb_kernel(
 
         input_terms = {}
 
-        def gate_products(ft):
+        def input_product(ft):
             cols = slice(ft * P, (ft + 1) * P)
             input_term = work.tile([P, BATCH_TILES, P], F32, name="input_term")
             nc.vector.tensor_tensor(out=input_term[:], in0=gate_cols[(ft, 0)][:], in1=i_sb[:, :, cols], op=ALU.mult)
-            nc.vector.tensor_tensor(out=readout[:, :, cols], in0=gate_cols[(ft, 1)][:], in1=readout[:, :, cols], op=ALU.mult)
             input_terms[ft] = input_term
+
+        def output_product(ft):
+            cols = slice(ft * P, (ft + 1) * P)
+            nc.vector.tensor_tensor(out=readout[:, :, cols], in0=gate_cols[(ft, 1)][:], in1=readout[:, :, cols], op=ALU.mult)
 
         def finish_cell(ft):
             cols = slice(ft * P, (ft + 1) * P)
@@ -245,23 +248,20 @@ def tile_slstmlayer_pb_kernel(
         for ft in range(0, FEATURE_TILES + 1):
             ahead = ft + 1
             behind = ft - 1
-            if ahead < FEATURE_TILES:
-                for gate in range(GATES):
+            for gate in range(GATES):
+                if ahead < FEATURE_TILES:
                     transpose_weights(ahead, gate)
-            if behind >= 0:
-                for gate in range(GATES):
+                if behind >= 0:
                     transpose_back(behind, gate)
-            if ahead < FEATURE_TILES:
-                quantise_weights(ahead, 0)
-            if behind >= 0:
-                gate_products(behind)
-                finish_cell(behind)
-            if ahead < FEATURE_TILES:
-                quantise_weights(ahead, 1)
+                if ahead < FEATURE_TILES:
+                    quantise_weights(ahead, gate)
+                if behind >= 0:
+                    (input_product, output_product)[gate](behind)
+                if gate == 1 and behind >= 0:
+                    finish_cell(behind)
+                if ft < FEATURE_TILES:
+                    multiply_and_activate(ft, gate)
             if behind >= 0:
                 finish_readout(behind)
-            if 0 <= ft < FEATURE_TILES:
-                for gate in range(GATES):
-                    multiply_and_activate(ft, gate)
             if ahead < FEATURE_TILES:
                 prepare_states(ahead)

@@ -42,23 +42,21 @@ def tile_slstmlayer_pb_kernel(
         keep = ctx.enter_context(tc.tile_pool(name="keep", bufs=1))
         regrouped = ctx.enter_context(tc.tile_pool(name="regrouped", bufs=4))
         quantised = ctx.enter_context(tc.tile_pool(name="quantised", bufs=4))
+        rows_pool = ctx.enter_context(tc.tile_pool(name="rows_pool", bufs=GATES * 2))
         work = ctx.enter_context(tc.tile_pool(name="work", bufs=2))
-        flipped_banks = ctx.enter_context(tc.psum_pool(name="flipped_banks", bufs=4))
-        product_banks = ctx.enter_context(tc.psum_pool(name="product_banks", bufs=2))
-        gate_banks = ctx.enter_context(tc.psum_pool(name="gate_banks", bufs=2))
+        banks = ctx.enter_context(tc.psum_pool(name="banks", bufs=8))
 
         identity = keep.tile([P, P], F32, name="identity")
-        act_raw = [keep.tile([P, BATCH_TILES * FEATURES], BF16, name="act_raw%d" % s) for s in range(SOURCES)]
+        act_raw = [keep.tile([P, BATCH_TILES, FEATURES], BF16, name="act_raw%d" % s) for s in range(SOURCES)]
         w_raw = [
-            [keep.tile([P, FEATURE_TILES * FEATURES], BF16, name="w_raw%d%d" % (gate, s)) for s in range(SOURCES)]
-            for gate in range(GATES)
+            keep.tile([P, FEATURE_TILES, SOURCES, FEATURES], BF16, name="w_raw%d" % gate) for gate in range(GATES)
         ]
         f_sb = keep.tile([P, BATCH_TILES, FEATURES], BF16, name="f_sb")
         n_sb = keep.tile([P, BATCH_TILES, FEATURES], BF16, name="n_sb")
         i_sb = keep.tile([P, BATCH_TILES, FEATURES], BF16, name="i_sb")
         c_sb = keep.tile([P, BATCH_TILES, FEATURES], BF16, name="c_sb")
         cell = keep.tile([P, BATCH_TILES, FEATURES], F32, name="cell")
-        readout = keep.tile([P, BATCH_TILES, FEATURES], F32, name="readout")
+        norm = keep.tile([P, BATCH_TILES, FEATURES], F32, name="norm")
         act_grouped = [
             keep.tile([P, SOURCE_PASSES * BATCH * PACK], BF16, name="act_grouped%d" % s, align_bytes=64)
             for s in range(SOURCES)
@@ -73,43 +71,43 @@ def tile_slstmlayer_pb_kernel(
         make_identity(nc, identity[:])
         bias_rows = keep.tile([P, P], BF16, name="bias_rows")
         nc.vector.memset(bias_rows[:], 0.0)
-        for gate, bias in enumerate((b_z, b_o)):
-            nc.scalar.dma_start(
-                out=bias_rows[gate * FEATURE_TILES : (gate + 1) * FEATURE_TILES, :],
-                in_=bias.rearrange("(r c) -> r c", c=P),
-            )
 
-        def load_weights(ft):
-            for gate, pair in enumerate(((Wz_x, Wz_h), (Wo_x, Wo_h))):
-                for s, dram in enumerate(pair):
+        def load_weights(ft, sources=(0, 1)):
+            for s in sources:
+                for gate, dram in enumerate(((Wz_x, Wo_x), (Wz_h, Wo_h))[s]):
                     nc.sync.dma_start(
-                        out=w_raw[gate][s][:, ft * FEATURES : (ft + 1) * FEATURES],
+                        out=w_raw[gate][:, ft, s, :],
                         in_=dram[ft * P : (ft + 1) * P, :],
                     )
 
-        def load_gates(tiles):
+        def load_rows(sbuf, dram, tiles=range(BATCH_TILES)):
             for t in tiles:
-                for sbuf, dram in ((f_sb, f_prime), (n_sb, n_prev)):
-                    nc.sync.dma_start(out=sbuf[:, t, :], in_=by_batch_tile(dram)[:, t, :])
-            for t in tiles:
-                nc.sync.dma_start(out=i_sb[:, t, :], in_=by_batch_tile(i_prime)[:, t, :])
+                nc.sync.dma_start(out=sbuf[:, t, :], in_=by_batch_tile(dram)[:, t, :])
 
-        def load_activations(s, dram):
-            nc.sync.dma_start(out=act_raw[s][:].rearrange("p (t f) -> p t f", t=BATCH_TILES), in_=by_batch_tile(dram))
-
-        load_gates(range(0, BATCH_TILES // 2))
-        load_activations(0, x)
-        load_gates(range(BATCH_TILES // 2, BATCH_TILES))
+        for t in (0, 1):
+            load_rows(f_sb, f_prime, (t,))
+            load_rows(n_sb, n_prev, (t,))
+        load_rows(act_raw[0], x, (0, 1))
+        load_rows(i_sb, i_prime, (0, 1))
+        load_rows(act_raw[0], x, (2, 3))
+        load_rows(f_sb, f_prime, (2, 3))
+        load_rows(n_sb, n_prev, (2, 3))
+        load_rows(i_sb, i_prime, (2, 3))
+        for gate, bias in enumerate((b_z, b_o)):
+            nc.sync.dma_start(
+                out=bias_rows[gate * FEATURE_TILES : (gate + 1) * FEATURE_TILES, :],
+                in_=bias.rearrange("(r c) -> r c", c=P),
+            )
         load_weights(0)
-        load_activations(1, h_prev)
+        load_rows(act_raw[1], h_prev)
         load_weights(1)
         load_weights(2)
-        nc.sync.dma_start(out=c_sb[:], in_=by_batch_tile(c_prev))
+        load_rows(c_sb, c_prev)
         for ft in range(3, FEATURE_TILES):
             load_weights(ft)
 
         def regroup_rows(words, grouped_words, on_vector=False):
-            bank = flipped_banks.tile([P, WORD_BLOCKS, P], F32, name="flipped")
+            bank = banks.tile([P, WORD_BLOCKS, P], F32, name="bank")
             for j in range(WORD_BLOCKS):
                 g, u = divmod(j, 2)
                 nc.tensor.transpose(bank[:, j, :], words[:, 2 * P * g + u : 2 * P * (g + 1) : 2], identity[:])
@@ -118,17 +116,17 @@ def tile_slstmlayer_pb_kernel(
             else:
                 nc.scalar.copy(out=grouped_words, in_=bank[:].rearrange("q (g u) r -> q g r u", u=2))
 
-        def normaliser(tiles):
-            for t in tiles:
-                nc.vector.tensor_tensor(out=readout[:, t, :], in0=f_sb[:, t, :], in1=n_sb[:, t, :], op=ALU.mult)
-            for t in tiles:
-                nc.vector.tensor_tensor(out=readout[:, t, :], in0=readout[:, t, :], in1=i_sb[:, t, :], op=ALU.add)
-            for t in tiles:
-                nc.vector.tensor_scalar_max(out=readout[:, t, :], in0=readout[:, t, :], scalar1=N_FLOOR)
+        def forget_products(t):
+            nc.vector.tensor_tensor(out=norm[:, t, :], in0=f_sb[:, t, :], in1=n_sb[:, t, :], op=ALU.mult)
 
-        def reciprocal_root(tiles):
-            for t in tiles:
-                nc.scalar.activation(out=readout[:, t, :], in_=readout[:, t, :], func=ACT.Abs_reciprocal_sqrt)
+        def normaliser_sum(t):
+            nc.vector.tensor_tensor(out=norm[:, t, :], in0=norm[:, t, :], in1=i_sb[:, t, :], op=ALU.add)
+
+        def clamp(t):
+            nc.vector.tensor_scalar_max(out=norm[:, t, :], in0=norm[:, t, :], scalar1=N_FLOOR)
+
+        def reciprocal_root(t):
+            nc.scalar.activation(out=norm[:, t, :], in_=norm[:, t, :], func=ACT.Abs_reciprocal_sqrt)
 
         def quantise_activations(s):
             for g in range(SOURCE_PASSES):
@@ -144,13 +142,13 @@ def tile_slstmlayer_pb_kernel(
         gate_rows = {}
         gate_cols = {}
 
-        def transpose_weights(ft, gate):
-            grouped = regrouped.tile([P, PASSES * P * PACK], BF16, name="w_grouped", align_bytes=64)
-            grouped_words = grouped[:].bitcast(F32).rearrange("q (s g r u) -> q s g r u", s=SOURCES, g=SOURCE_PASSES, u=2)
-            for s in range(SOURCES):
-                words = w_raw[gate][s][:].bitcast(F32)[:, ft * WORDS : (ft + 1) * WORDS]
-                regroup_rows(words, grouped_words[:, s])
-            w_grouped[(ft, gate)] = grouped
+        def transpose_weights(ft, gate, s):
+            if s == 0:
+                w_grouped[(ft, gate)] = regrouped.tile([P, PASSES * P * PACK], BF16, name="w_grouped", align_bytes=64)
+            grouped_words = w_grouped[(ft, gate)][:].bitcast(F32).rearrange(
+                "q (s g r u) -> q s g r u", s=SOURCES, g=SOURCE_PASSES, u=2
+            )
+            regroup_rows(w_raw[gate][:].bitcast(F32)[:, ft, s], grouped_words[:, s])
 
         def quantise_weights(ft, gate):
             codes = quantised.tile([P, PASSES * P], U32, name="w_codes", align_bytes=64)
@@ -159,8 +157,10 @@ def tile_slstmlayer_pb_kernel(
             w_codes[(ft, gate)] = codes
             w_scales[(ft, gate)] = scales
 
-        def multiply_and_activate(ft, gate):
-            product = product_banks.tile([P, BATCH], F32, name="product")
+        products = {}
+
+        def multiply(ft, gate):
+            product = banks.tile([P, BATCH], F32, name="bank")
             for k in range(PASSES):
                 columns = slice(k * P, (k + 1) * P)
                 nc.tensor.matmul_mx(
@@ -172,29 +172,34 @@ def tile_slstmlayer_pb_kernel(
                     start=(k == 0),
                     stop=(k == PASSES - 1),
                 )
-            rows = work.tile([P, BATCH], F32, name="gate_rows")
+            products[(ft, gate)] = product
+
+        def activate(ft, gate):
+            rows = rows_pool.tile([P, BATCH], F32, name="gate_rows")
             column = gate * FEATURE_TILES + ft
             nc.scalar.activation(
-                out=rows[:], in_=product[:], func=gate_function[gate], bias=bias_cols[:, column : column + 1]
+                out=rows[:], in_=products[(ft, gate)][:], func=gate_function[gate], bias=bias_cols[:, column : column + 1]
             )
             gate_rows[(ft, gate)] = rows
 
         def transpose_back(ft, gate):
-            bank = gate_banks.tile([P, BATCH_TILES, P], F32, name="gate_cols")
+            bank = banks.tile([P, BATCH_TILES, P], F32, name="bank")
             for t in range(BATCH_TILES):
                 nc.tensor.transpose(bank[:, t, :], gate_rows[(ft, gate)][:, t * P : (t + 1) * P], identity[:])
             gate_cols[(ft, gate)] = bank
 
         kept_terms = {}
+        input_terms = {}
 
-        def prepare_states(ft):
+        def kept_product(ft):
             cols = slice(ft * P, (ft + 1) * P)
-            nc.scalar.activation(out=readout[:, :, cols], in_=readout[:, :, cols], func=ACT.Square)
             kept = work.tile([P, BATCH_TILES, P], F32, name="kept_term")
-            nc.gpsimd.tensor_tensor(out=kept[:], in0=f_sb[:, :, cols], in1=c_sb[:, :, cols], op=ALU.mult)
+            nc.vector.tensor_tensor(out=kept[:], in0=f_sb[:, :, cols], in1=c_sb[:, :, cols], op=ALU.mult)
             kept_terms[ft] = kept
 
-        input_terms = {}
+        def reciprocal(ft):
+            cols = slice(ft * P, (ft + 1) * P)
+            nc.scalar.activation(out=norm[:, :, cols], in_=norm[:, :, cols], func=ACT.Square)
 
         def input_product(ft):
             cols = slice(ft * P, (ft + 1) * P)
@@ -202,66 +207,81 @@ def tile_slstmlayer_pb_kernel(
             nc.vector.tensor_tensor(out=input_term[:], in0=gate_cols[(ft, 0)][:], in1=i_sb[:, :, cols], op=ALU.mult)
             input_terms[ft] = input_term
 
-        def output_product(ft):
-            cols = slice(ft * P, (ft + 1) * P)
-            nc.vector.tensor_tensor(out=readout[:, :, cols], in0=gate_cols[(ft, 1)][:], in1=readout[:, :, cols], op=ALU.mult)
-
         def finish_cell(ft):
             cols = slice(ft * P, (ft + 1) * P)
             nc.vector.tensor_tensor(out=cell[:, :, cols], in0=input_terms[ft][:], in1=kept_terms[ft][:], op=ALU.add)
             nc.sync.dma_start(out=by_batch_tile(out_1)[:, :, cols], in_=cell[:, :, cols])
 
+        def output_product(ft):
+            cols = slice(ft * P, (ft + 1) * P)
+            nc.vector.tensor_tensor(out=norm[:, :, cols], in0=gate_cols[(ft, 1)][:], in1=norm[:, :, cols], op=ALU.mult)
+
         def finish_readout(ft):
             cols = slice(ft * P, (ft + 1) * P)
-            nc.vector.tensor_tensor(out=readout[:, :, cols], in0=readout[:, :, cols], in1=cell[:, :, cols], op=ALU.mult)
-            nc.sync.dma_start(out=by_batch_tile(out_0)[:, :, cols], in_=readout[:, :, cols])
+            nc.vector.tensor_tensor(out=norm[:, :, cols], in0=norm[:, :, cols], in1=cell[:, :, cols], op=ALU.mult)
+            nc.sync.dma_start(out=by_batch_tile(out_0)[:, :, cols], in_=norm[:, :, cols])
 
-        def regroup_activations(s):
-            words = act_raw[s][:].bitcast(F32).rearrange("p (t w) -> p t w", t=BATCH_TILES)
+        def regroup_activations(s, vector_tiles=()):
+            words = act_raw[s][:].bitcast(F32)
             grouped_words = act_grouped[s][:].bitcast(F32).rearrange(
                 "q (g t r u) -> q g t r u", g=SOURCE_PASSES, t=BATCH_TILES, u=2
             )
             for t in range(BATCH_TILES):
-                regroup_rows(words[:, t, :], grouped_words[:, :, t], on_vector=(s == SOURCES - 1 and t % 2 == 1))
+                regroup_rows(words[:, t, :], grouped_words[:, :, t], on_vector=(t in vector_tiles))
 
-        normaliser(range(0, BATCH_TILES // 2))
+        def normaliser(tiles):
+            for step in (forget_products, normaliser_sum, clamp):
+                for t in tiles:
+                    step(t)
+
+        normaliser((0, 1))
         regroup_activations(0)
-        reciprocal_root(range(0, BATCH_TILES // 2))
+        reciprocal_root(0)
+        reciprocal_root(1)
+        quantise_activations(0)
+        normaliser((2, 3))
         bias_rows_f32 = keep.tile([P, P], F32, name="bias_rows_f32")
         nc.vector.tensor_copy(out=bias_rows_f32[:], in_=bias_rows[:])
-        bias_bank = flipped_banks.tile([P, WORD_BLOCKS, P], F32, name="flipped")
-        nc.tensor.transpose(bias_bank[:, 0, :], bias_rows_f32[:], identity[:])
-        bias_cols = keep.tile([P, GATES * FEATURE_TILES], F32, name="bias_cols")
-        nc.vector.tensor_copy(out=bias_cols[:], in_=bias_bank[:, 0, 0 : GATES * FEATURE_TILES])
-        normaliser(range(BATCH_TILES // 2, BATCH_TILES))
-        quantise_activations(0)
         for gate in range(GATES):
-            transpose_weights(0, gate)
-        reciprocal_root(range(BATCH_TILES // 2, BATCH_TILES))
-        nc.scalar.activation(out=warm[:], in_=ones[:], func=ACT.Sigmoid)
+            for s in range(SOURCES):
+                transpose_weights(0, gate, s)
         for gate in range(GATES):
             quantise_weights(0, gate)
-        regroup_activations(1)
+        regroup_activations(1, (1, 3))
+        reciprocal_root(2)
+        reciprocal_root(3)
+        nc.scalar.activation(out=warm[:], in_=ones[:], func=ACT.Sigmoid)
+        bias_bank = banks.tile([P, BATCH_TILES, P], F32, name="bank")
+        nc.tensor.transpose(bias_bank[:, 0, :], bias_rows_f32[:], identity[:])
+        bias_cols = keep.tile([P, GATES * FEATURE_TILES], F32, name="bias_cols")
         quantise_activations(1)
-        prepare_states(0)
+        nc.vector.tensor_copy(out=bias_cols[:], in_=bias_bank[:, 0, 0 : GATES * FEATURE_TILES])
 
         for ft in range(0, FEATURE_TILES + 1):
             ahead = ft + 1
             behind = ft - 1
+            if behind >= 0:
+                kept_product(behind)
+            if behind >= 1:
+                finish_readout(behind - 1)
             for gate in range(GATES):
                 if ahead < FEATURE_TILES:
-                    transpose_weights(ahead, gate)
+                    for s in range(SOURCES):
+                        transpose_weights(ahead, gate, s)
                 if behind >= 0:
                     transpose_back(behind, gate)
+                    if gate == 0:
+                        input_product(behind)
+                    else:
+                        finish_cell(behind)
+                        output_product(behind)
                 if ahead < FEATURE_TILES:
                     quantise_weights(ahead, gate)
-                if behind >= 0:
-                    (input_product, output_product)[gate](behind)
-                if gate == 1 and behind >= 0:
-                    finish_cell(behind)
                 if ft < FEATURE_TILES:
-                    multiply_and_activate(ft, gate)
-            if behind >= 0:
-                finish_readout(behind)
+                    multiply(ft, gate)
+                    activate(ft, gate)
+            if ft == 0:
+                reciprocal(0)
             if ahead < FEATURE_TILES:
-                prepare_states(ahead)
+                reciprocal(ahead)
+        finish_readout(FEATURE_TILES - 1)

@@ -44,6 +44,7 @@ def tile_slstmlayer_pb_kernel(
         quantised = ctx.enter_context(tc.tile_pool(name="quantised", bufs=4))
         rows_pool = ctx.enter_context(tc.tile_pool(name="rows_pool", bufs=GATES * 2))
         work = ctx.enter_context(tc.tile_pool(name="work", bufs=2))
+        sorted_pool = ctx.enter_context(tc.tile_pool(name="sorted_pool", bufs=GATES * 2))
         banks = ctx.enter_context(tc.psum_pool(name="banks", bufs=8))
 
         identity = keep.tile([P, P], F32, name="identity")
@@ -84,21 +85,25 @@ def tile_slstmlayer_pb_kernel(
             for t in tiles:
                 nc.sync.dma_start(out=sbuf[:, t, :], in_=by_batch_tile(dram)[:, t, :])
 
-        for t in (0, 1):
-            load_rows(f_sb, f_prime, (t,))
-            load_rows(n_sb, n_prev, (t,))
-        load_rows(act_raw[0], x, (0, 1))
-        load_rows(i_sb, i_prime, (0, 1))
-        load_rows(act_raw[0], x, (2, 3))
-        load_rows(f_sb, f_prime, (2, 3))
-        load_rows(n_sb, n_prev, (2, 3))
-        load_rows(i_sb, i_prime, (2, 3))
+        load_rows(f_sb, f_prime, (0,))
+        load_rows(n_sb, n_prev, (0,))
         for gate, bias in enumerate((b_z, b_o)):
             nc.sync.dma_start(
                 out=bias_rows[gate * FEATURE_TILES : (gate + 1) * FEATURE_TILES, :],
                 in_=bias.rearrange("(r c) -> r c", c=P),
             )
-        load_weights(0)
+        load_rows(f_sb, f_prime, (1,))
+        load_rows(n_sb, n_prev, (1,))
+        load_rows(act_raw[0], x, (0, 1))
+        load_rows(i_sb, i_prime, (0, 1))
+        load_rows(act_raw[0], x, (2, 3))
+        load_weights(0, (0,))
+        load_rows(f_sb, f_prime, (2,))
+        load_rows(n_sb, n_prev, (2,))
+        load_weights(0, (1,))
+        load_rows(f_sb, f_prime, (3,))
+        load_rows(n_sb, n_prev, (3,))
+        load_rows(i_sb, i_prime, (2, 3))
         load_rows(act_raw[1], h_prev)
         load_weights(1)
         load_weights(2)
@@ -106,15 +111,31 @@ def tile_slstmlayer_pb_kernel(
         for ft in range(3, FEATURE_TILES):
             load_weights(ft)
 
-        def regroup_rows(words, grouped_words, on_vector=False):
+
+        def regroup_rows(words, grouped_words, is_sorted=False, on_vector=False):
             bank = banks.tile([P, WORD_BLOCKS, P], F32, name="bank")
             for j in range(WORD_BLOCKS):
                 g, u = divmod(j, 2)
-                nc.tensor.transpose(bank[:, j, :], words[:, 2 * P * g + u : 2 * P * (g + 1) : 2], identity[:])
+                block = words[:, j * P : (j + 1) * P] if is_sorted else words[:, 2 * P * g + u : 2 * P * (g + 1) : 2]
+                nc.tensor.transpose(bank[:, j, :], block, identity[:])
             if on_vector:
                 nc.vector.tensor_copy(out=grouped_words, in_=bank[:].rearrange("q (g u) r -> q g r u", u=2))
             else:
                 nc.scalar.copy(out=grouped_words, in_=bank[:].rearrange("q (g u) r -> q g r u", u=2))
+
+        w_sorted = {}
+        sorted_sources = {}
+
+        def sort_weights(ft, gate, sources, on_vector):
+            w_sorted[(ft, gate)] = sorted_pool.tile([P, SOURCES, FEATURES], BF16, name="w_sorted")
+            sorted_sources[(ft, gate)] = sources
+            which = slice(sources[0], sources[-1] + 1)
+            out = w_sorted[(ft, gate)][:].bitcast(F32)[:, which].rearrange("r s (g u q) -> r (s g) u q", g=SOURCE_PASSES, u=2)
+            raw = w_raw[gate][:].bitcast(F32)[:, ft, which].rearrange("r s (g q u) -> r (s g) u q", g=SOURCE_PASSES, u=2)
+            if on_vector:
+                nc.vector.tensor_copy(out=out, in_=raw)
+            else:
+                nc.scalar.copy(out=out, in_=raw)
 
         def forget_products(t):
             nc.vector.tensor_tensor(out=norm[:, t, :], in0=f_sb[:, t, :], in1=n_sb[:, t, :], op=ALU.mult)
@@ -142,13 +163,15 @@ def tile_slstmlayer_pb_kernel(
         gate_rows = {}
         gate_cols = {}
 
-        def transpose_weights(ft, gate, s):
+        def transpose_weights(ft, gate, s, on_vector=False):
             if s == 0:
                 w_grouped[(ft, gate)] = regrouped.tile([P, PASSES * P * PACK], BF16, name="w_grouped", align_bytes=64)
             grouped_words = w_grouped[(ft, gate)][:].bitcast(F32).rearrange(
                 "q (s g r u) -> q s g r u", s=SOURCES, g=SOURCE_PASSES, u=2
             )
-            regroup_rows(w_raw[gate][:].bitcast(F32)[:, ft, s], grouped_words[:, s])
+            is_sorted = s in sorted_sources.get((ft, gate), ())
+            words = w_sorted[(ft, gate)][:, s] if is_sorted else w_raw[gate][:, ft, s]
+            regroup_rows(words.bitcast(F32), grouped_words[:, s], is_sorted, on_vector)
 
         def quantise_weights(ft, gate):
             codes = quantised.tile([P, PASSES * P], U32, name="w_codes", align_bytes=64)
@@ -236,30 +259,38 @@ def tile_slstmlayer_pb_kernel(
 
         normaliser((0, 1))
         regroup_activations(0)
-        reciprocal_root(0)
-        reciprocal_root(1)
-        quantise_activations(0)
-        normaliser((2, 3))
         bias_rows_f32 = keep.tile([P, P], F32, name="bias_rows_f32")
         nc.vector.tensor_copy(out=bias_rows_f32[:], in_=bias_rows[:])
-        for gate in range(GATES):
-            for s in range(SOURCES):
-                transpose_weights(0, gate, s)
-        for gate in range(GATES):
-            quantise_weights(0, gate)
-        regroup_activations(1, (1, 3))
-        reciprocal_root(2)
-        reciprocal_root(3)
-        nc.scalar.activation(out=warm[:], in_=ones[:], func=ACT.Sigmoid)
         bias_bank = banks.tile([P, BATCH_TILES, P], F32, name="bank")
         nc.tensor.transpose(bias_bank[:, 0, :], bias_rows_f32[:], identity[:])
         bias_cols = keep.tile([P, GATES * FEATURE_TILES], F32, name="bias_cols")
-        quantise_activations(1)
+        reciprocal_root(0)
+        reciprocal_root(1)
+        for s in range(SOURCES):
+            for gate in range(GATES):
+                transpose_weights(0, gate, s)
+        quantise_activations(0)
         nc.vector.tensor_copy(out=bias_cols[:], in_=bias_bank[:, 0, 0 : GATES * FEATURE_TILES])
+        forget_products(2)
+        forget_products(3)
+        normaliser_sum(2)
+        for gate in range(GATES):
+            quantise_weights(0, gate)
+        normaliser_sum(3)
+        clamp(2)
+        clamp(3)
+        regroup_activations(1, ())
+        reciprocal_root(2)
+        reciprocal_root(3)
+        nc.scalar.activation(out=warm[:], in_=ones[:], func=ACT.Sigmoid)
+        quantise_activations(1)
 
         for ft in range(0, FEATURE_TILES + 1):
             ahead = ft + 1
             behind = ft - 1
+            if 0 <= ft and ahead + 1 < FEATURE_TILES:
+                sort_weights(ahead + 1, 0, (0, 1), on_vector=True)
+                sort_weights(ahead + 1, 1, (0,), on_vector=False)
             if behind >= 0:
                 kept_product(behind)
             if behind >= 1:
@@ -267,7 +298,7 @@ def tile_slstmlayer_pb_kernel(
             for gate in range(GATES):
                 if ahead < FEATURE_TILES:
                     for s in range(SOURCES):
-                        transpose_weights(ahead, gate, s)
+                        transpose_weights(ahead, gate, s, on_vector=(ft == 0))
                 if behind >= 0:
                     transpose_back(behind, gate)
                     if gate == 0:

@@ -81,33 +81,31 @@ def tile_slstmlayer_pb_kernel(
                         in_=dram[ft * P : (ft + 1) * P, :],
                     )
 
-        def load_rows(sbuf, dram, tiles=range(BATCH_TILES)):
-            for t in tiles:
-                nc.sync.dma_start(out=sbuf[:, t, :], in_=by_batch_tile(dram)[:, t, :])
+        def load_rows(sbuf, dram, first, last):
+            nc.sync.dma_start(out=sbuf[:, first:last, :], in_=by_batch_tile(dram)[:, first:last, :])
 
-        load_rows(f_sb, f_prime, (0,))
-        load_rows(n_sb, n_prev, (0,))
+        load_rows(f_sb, f_prime, 0, 1)
+        load_rows(n_sb, n_prev, 0, 1)
         for gate, bias in enumerate((b_z, b_o)):
             nc.sync.dma_start(
                 out=bias_rows[gate * FEATURE_TILES : (gate + 1) * FEATURE_TILES, :],
                 in_=bias.rearrange("(r c) -> r c", c=P),
             )
-        load_rows(f_sb, f_prime, (1,))
-        load_rows(n_sb, n_prev, (1,))
-        load_rows(act_raw[0], x, (0, 1))
-        load_rows(i_sb, i_prime, (0, 1))
-        load_rows(act_raw[0], x, (2, 3))
+        load_rows(f_sb, f_prime, 1, 2)
+        load_rows(n_sb, n_prev, 1, 2)
+        load_rows(act_raw[0], x, 0, 2)
+        load_rows(i_sb, i_prime, 0, 2)
+        load_rows(act_raw[0], x, 2, 4)
         load_weights(0, (0,))
-        load_rows(f_sb, f_prime, (2,))
-        load_rows(n_sb, n_prev, (2,))
+        load_rows(f_sb, f_prime, 2, 4)
+        load_rows(n_sb, n_prev, 2, 4)
         load_weights(0, (1,))
-        load_rows(f_sb, f_prime, (3,))
-        load_rows(n_sb, n_prev, (3,))
-        load_rows(i_sb, i_prime, (2, 3))
-        load_rows(act_raw[1], h_prev)
+        load_rows(i_sb, i_prime, 2, 4)
+        load_rows(act_raw[1], h_prev, 0, 2)
+        load_rows(act_raw[1], h_prev, 2, 4)
         load_weights(1)
         load_weights(2)
-        load_rows(c_sb, c_prev)
+        load_rows(c_sb, c_prev, 0, 4)
         for ft in range(3, FEATURE_TILES):
             load_weights(ft)
 
@@ -182,28 +180,33 @@ def tile_slstmlayer_pb_kernel(
 
         products = {}
 
-        def multiply(ft, gate):
-            product = banks.tile([P, BATCH], F32, name="bank")
+        def multiply(ft, gate, first=0, last=BATCH_TILES):
+            if first == 0:
+                products[(ft, gate)] = banks.tile([P, BATCH], F32, name="bank")
+            batch = slice(first * P, last * P)
             for k in range(PASSES):
                 columns = slice(k * P, (k + 1) * P)
                 nc.tensor.matmul_mx(
-                    out=product[:],
+                    out=products[(ft, gate)][:, batch],
                     lhsT=w_codes[(ft, gate)][:, columns].bitcast(FP8X4),
                     lhsT_scale=w_scales[(ft, gate)][:, columns],
-                    rhs=act_codes[:, k, :].bitcast(FP8X4),
-                    rhs_scale=act_scales[:, k, :],
+                    rhs=act_codes[:, k, batch].bitcast(FP8X4),
+                    rhs_scale=act_scales[:, k, batch],
                     start=(k == 0),
                     stop=(k == PASSES - 1),
                 )
-            products[(ft, gate)] = product
 
-        def activate(ft, gate):
-            rows = rows_pool.tile([P, BATCH], F32, name="gate_rows")
+        def activate(ft, gate, first=0, last=BATCH_TILES):
+            if first == 0:
+                gate_rows[(ft, gate)] = rows_pool.tile([P, BATCH], F32, name="gate_rows")
+            batch = slice(first * P, last * P)
             column = gate * FEATURE_TILES + ft
             nc.scalar.activation(
-                out=rows[:], in_=products[(ft, gate)][:], func=gate_function[gate], bias=bias_cols[:, column : column + 1]
+                out=gate_rows[(ft, gate)][:, batch],
+                in_=products[(ft, gate)][:, batch],
+                func=gate_function[gate],
+                bias=bias_cols[:, column : column + 1],
             )
-            gate_rows[(ft, gate)] = rows
 
         def transpose_back(ft, gate):
             bank = banks.tile([P, BATCH_TILES, P], F32, name="bank")
@@ -235,14 +238,14 @@ def tile_slstmlayer_pb_kernel(
             nc.vector.tensor_tensor(out=cell[:, :, cols], in0=input_terms[ft][:], in1=kept_terms[ft][:], op=ALU.add)
             nc.sync.dma_start(out=by_batch_tile(out_1)[:, :, cols], in_=cell[:, :, cols])
 
-        def output_product(ft):
-            cols = slice(ft * P, (ft + 1) * P)
-            nc.vector.tensor_tensor(out=norm[:, :, cols], in0=gate_cols[(ft, 1)][:], in1=norm[:, :, cols], op=ALU.mult)
+        def output_product(ft, first=0, last=BATCH_TILES):
+            part = (slice(None), slice(first, last), slice(ft * P, (ft + 1) * P))
+            nc.vector.tensor_tensor(out=norm[part], in0=gate_cols[(ft, 1)][:, first:last, :], in1=norm[part], op=ALU.mult)
 
-        def finish_readout(ft):
-            cols = slice(ft * P, (ft + 1) * P)
-            nc.vector.tensor_tensor(out=norm[:, :, cols], in0=norm[:, :, cols], in1=cell[:, :, cols], op=ALU.mult)
-            nc.sync.dma_start(out=by_batch_tile(out_0)[:, :, cols], in_=norm[:, :, cols])
+        def finish_readout(ft, first=0, last=BATCH_TILES):
+            part = (slice(None), slice(first, last), slice(ft * P, (ft + 1) * P))
+            nc.vector.tensor_tensor(out=norm[part], in0=norm[part], in1=cell[part], op=ALU.mult)
+            nc.sync.dma_start(out=by_batch_tile(out_0)[part], in_=norm[part])
 
         def regroup_activations(s, vector_tiles=()):
             words = act_raw[s][:].bitcast(F32)
@@ -252,12 +255,9 @@ def tile_slstmlayer_pb_kernel(
             for t in range(BATCH_TILES):
                 regroup_rows(words[:, t, :], grouped_words[:, :, t], on_vector=(t in vector_tiles))
 
-        def normaliser(tiles):
-            for step in (forget_products, normaliser_sum, clamp):
-                for t in tiles:
-                    step(t)
-
-        normaliser((0, 1))
+        for step in (forget_products, normaliser_sum, clamp):
+            for t in (0, 1):
+                step(t)
         regroup_activations(0)
         bias_rows_f32 = keep.tile([P, P], F32, name="bias_rows_f32")
         nc.vector.tensor_copy(out=bias_rows_f32[:], in_=bias_rows[:])
@@ -285,34 +285,53 @@ def tile_slstmlayer_pb_kernel(
         nc.scalar.activation(out=warm[:], in_=ones[:], func=ACT.Sigmoid)
         quantise_activations(1)
 
-        for ft in range(0, FEATURE_TILES + 1):
+        def transposes(ft, gate):
             ahead = ft + 1
             behind = ft - 1
-            if 0 <= ft and ahead + 1 < FEATURE_TILES:
-                sort_weights(ahead + 1, 0, (0, 1), on_vector=True)
-                sort_weights(ahead + 1, 1, (0,), on_vector=False)
+            if ahead < FEATURE_TILES:
+                for s in range(SOURCES):
+                    transpose_weights(ahead, gate, s, on_vector=(ft == 0))
             if behind >= 0:
-                kept_product(behind)
-            if behind >= 1:
-                finish_readout(behind - 1)
+                transpose_back(behind, gate)
+                if gate == 0:
+                    input_product(behind)
+                else:
+                    finish_cell(behind)
+                    output_product(behind)
+            if ahead < FEATURE_TILES:
+                quantise_weights(ahead, gate)
+
+        for ft in range(FEATURE_TILES):
+            if 1 <= ft < FEATURE_TILES - 2:
+                sort_weights(ft + 2, 1, (0,), on_vector=True)
+                sort_weights(ft + 2, 0, (0,), on_vector=False)
+            if ft >= 1:
+                kept_product(ft - 1)
+            if ft >= 2:
+                finish_readout(ft - 2)
             for gate in range(GATES):
-                if ahead < FEATURE_TILES:
-                    for s in range(SOURCES):
-                        transpose_weights(ahead, gate, s, on_vector=(ft == 0))
-                if behind >= 0:
-                    transpose_back(behind, gate)
-                    if gate == 0:
-                        input_product(behind)
-                    else:
-                        finish_cell(behind)
-                        output_product(behind)
-                if ahead < FEATURE_TILES:
-                    quantise_weights(ahead, gate)
-                if ft < FEATURE_TILES:
+                transposes(ft, gate)
+            for gate in range(GATES):
+                if ft < FEATURE_TILES - 1 or gate == 0:
                     multiply(ft, gate)
                     activate(ft, gate)
             if ft == 0:
                 reciprocal(0)
-            if ahead < FEATURE_TILES:
-                reciprocal(ahead)
-        finish_readout(FEATURE_TILES - 1)
+            if ft < FEATURE_TILES - 1:
+                reciprocal(ft + 1)
+
+        last = FEATURE_TILES - 1
+        finish_readout(last - 1)
+        kept_product(last)
+        multiply(last, 1, 0, 2)
+        activate(last, 1, 0, 2)
+        transpose_back(last, 0)
+        input_product(last)
+        finish_cell(last)
+        multiply(last, 1, 2, 4)
+        activate(last, 1, 2, 4)
+        transpose_back(last, 1)
+        for half in (0, 2):
+            output_product(last, half, half + 2)
+        for half in (0, 2):
+            finish_readout(last, half, half + 2)

@@ -290,7 +290,7 @@ def tile_slstmlayer_pb_kernel(
             behind = ft - 1
             if ahead < FEATURE_TILES:
                 for s in range(SOURCES):
-                    transpose_weights(ahead, gate, s, on_vector=(ft == 0))
+                    transpose_weights(ahead, gate, s, on_vector=(ft == 0 and gate == 0))
             if behind >= 0:
                 transpose_back(behind, gate)
                 if gate == 0:
@@ -303,7 +303,6 @@ def tile_slstmlayer_pb_kernel(
 
         for ft in range(FEATURE_TILES):
             if 1 <= ft < FEATURE_TILES - 2:
-                sort_weights(ft + 2, 1, (0,), on_vector=True)
                 sort_weights(ft + 2, 0, (0,), on_vector=False)
             if ft >= 1:
                 kept_product(ft - 1)
@@ -311,7 +310,6 @@ def tile_slstmlayer_pb_kernel(
                 finish_readout(ft - 2)
             for gate in range(GATES):
                 transposes(ft, gate)
-            for gate in range(GATES):
                 if ft < FEATURE_TILES - 1 or gate == 0:
                     multiply(ft, gate)
                     activate(ft, gate)

@@ -24,6 +24,7 @@ WORDS = FEATURES // 2
 WORD_BLOCKS = WORDS // P
 GATES = 2
 N_FLOOR = 1e-6
+SORTED = (1, 0)
 
 FLOPS = 2 * BATCH * (SOURCES * FEATURES) * (GATES * FEATURES)
 
@@ -37,14 +38,15 @@ def tile_slstmlayer_pb_kernel(
     def by_batch_tile(dram):
         return dram.rearrange("(p t) f -> p t f", t=BATCH_TILES)
 
+    def feature_columns(first, last):
+        return (slice(None), slice(None), slice(first * P, last * P))
+
     with ExitStack() as ctx:
         ctx.enter_context(tc.manual_schedule())
         keep = ctx.enter_context(tc.tile_pool(name="keep", bufs=1))
-        regrouped = ctx.enter_context(tc.tile_pool(name="regrouped", bufs=4))
-        quantised = ctx.enter_context(tc.tile_pool(name="quantised", bufs=4))
-        rows_pool = ctx.enter_context(tc.tile_pool(name="rows_pool", bufs=GATES * 2))
+        weights = ctx.enter_context(tc.tile_pool(name="weights", bufs=2))
         work = ctx.enter_context(tc.tile_pool(name="work", bufs=2))
-        sorted_pool = ctx.enter_context(tc.tile_pool(name="sorted_pool", bufs=GATES * 2))
+        rows_pool = ctx.enter_context(tc.tile_pool(name="rows_pool", bufs=2 * GATES))
         banks = ctx.enter_context(tc.psum_pool(name="banks", bufs=8))
 
         identity = keep.tile([P, P], F32, name="identity")
@@ -62,8 +64,8 @@ def tile_slstmlayer_pb_kernel(
             keep.tile([P, SOURCE_PASSES * BATCH * PACK], BF16, name="act_grouped%d" % s, align_bytes=64)
             for s in range(SOURCES)
         ]
-        act_codes = keep.tile([P, PASSES, BATCH], U32, name="act_codes", align_bytes=64)
-        act_scales = keep.tile([P, PASSES, BATCH], U8, name="act_scales", align_bytes=64)
+        act_codes = keep.tile([P, PASSES * BATCH], U32, name="act_codes", align_bytes=64)
+        act_scales = keep.tile([P, PASSES * BATCH], U8, name="act_scales", align_bytes=64)
 
         ones = keep.tile([P, 1], F32, name="ones")
         warm = keep.tile([P, 1], F32, name="warm")
@@ -71,15 +73,12 @@ def tile_slstmlayer_pb_kernel(
         nc.scalar.activation(out=warm[:], in_=ones[:], func=ACT.Abs_reciprocal_sqrt)
         make_identity(nc, identity[:])
         bias_rows = keep.tile([P, P], BF16, name="bias_rows")
-        nc.vector.memset(bias_rows[:], 0.0)
+        nc.gpsimd.memset(bias_rows[:], 0.0)
 
         def load_weights(ft, sources=(0, 1)):
             for s in sources:
                 for gate, dram in enumerate(((Wz_x, Wo_x), (Wz_h, Wo_h))[s]):
-                    nc.sync.dma_start(
-                        out=w_raw[gate][:, ft, s, :],
-                        in_=dram[ft * P : (ft + 1) * P, :],
-                    )
+                    nc.sync.dma_start(out=w_raw[gate][:, ft, s, :], in_=dram[ft * P : (ft + 1) * P, :])
 
         def load_rows(sbuf, dram, first, last):
             nc.sync.dma_start(out=sbuf[:, first:last, :], in_=by_batch_tile(dram)[:, first:last, :])
@@ -93,8 +92,8 @@ def tile_slstmlayer_pb_kernel(
             )
         load_rows(f_sb, f_prime, 1, 2)
         load_rows(n_sb, n_prev, 1, 2)
-        load_rows(act_raw[0], x, 0, 2)
         load_rows(i_sb, i_prime, 0, 2)
+        load_rows(act_raw[0], x, 0, 2)
         load_rows(act_raw[0], x, 2, 4)
         load_weights(0, (0,))
         load_rows(f_sb, f_prime, 2, 4)
@@ -109,89 +108,95 @@ def tile_slstmlayer_pb_kernel(
         for ft in range(3, FEATURE_TILES):
             load_weights(ft)
 
-
         def regroup_rows(words, grouped_words, is_sorted=False, on_vector=False):
             bank = banks.tile([P, WORD_BLOCKS, P], F32, name="bank")
             for j in range(WORD_BLOCKS):
                 g, u = divmod(j, 2)
                 block = words[:, j * P : (j + 1) * P] if is_sorted else words[:, 2 * P * g + u : 2 * P * (g + 1) : 2]
                 nc.tensor.transpose(bank[:, j, :], block, identity[:])
-            if on_vector:
-                nc.vector.tensor_copy(out=grouped_words, in_=bank[:].rearrange("q (g u) r -> q g r u", u=2))
-            else:
-                nc.scalar.copy(out=grouped_words, in_=bank[:].rearrange("q (g u) r -> q g r u", u=2))
+            copy = nc.vector.tensor_copy if on_vector else nc.scalar.copy
+            copy(out=grouped_words, in_=bank[:].rearrange("q (g u) r -> q g r u", u=2))
 
-        w_sorted = {}
-        sorted_sources = {}
+        def forget_products(first, last):
+            part = (slice(None), slice(first, last))
+            nc.vector.tensor_tensor(out=norm[part], in0=f_sb[part], in1=n_sb[part], op=ALU.mult)
 
-        def sort_weights(ft, gate, sources, on_vector):
-            w_sorted[(ft, gate)] = sorted_pool.tile([P, SOURCES, FEATURES], BF16, name="w_sorted")
-            sorted_sources[(ft, gate)] = sources
-            which = slice(sources[0], sources[-1] + 1)
-            out = w_sorted[(ft, gate)][:].bitcast(F32)[:, which].rearrange("r s (g u q) -> r (s g) u q", g=SOURCE_PASSES, u=2)
-            raw = w_raw[gate][:].bitcast(F32)[:, ft, which].rearrange("r s (g q u) -> r (s g) u q", g=SOURCE_PASSES, u=2)
-            if on_vector:
-                nc.vector.tensor_copy(out=out, in_=raw)
-            else:
-                nc.scalar.copy(out=out, in_=raw)
+        def normaliser_sum(first, last):
+            part = (slice(None), slice(first, last))
+            nc.vector.tensor_tensor(out=norm[part], in0=norm[part], in1=i_sb[part], op=ALU.add)
 
-        def forget_products(t):
-            nc.vector.tensor_tensor(out=norm[:, t, :], in0=f_sb[:, t, :], in1=n_sb[:, t, :], op=ALU.mult)
-
-        def normaliser_sum(t):
-            nc.vector.tensor_tensor(out=norm[:, t, :], in0=norm[:, t, :], in1=i_sb[:, t, :], op=ALU.add)
-
-        def clamp(t):
-            nc.vector.tensor_scalar_max(out=norm[:, t, :], in0=norm[:, t, :], scalar1=N_FLOOR)
+        def clamp(first, last):
+            part = (slice(None), slice(first, last))
+            nc.vector.tensor_scalar_max(out=norm[part], in0=norm[part], scalar1=N_FLOOR)
 
         def reciprocal_root(t):
             nc.scalar.activation(out=norm[:, t, :], in_=norm[:, t, :], func=ACT.Abs_reciprocal_sqrt)
 
-        def quantise_activations(s):
-            for g in range(SOURCE_PASSES):
-                nc.vector.quantize_mx(
-                    out=act_codes[:, s * SOURCE_PASSES + g, :].bitcast(FP8X4),
-                    scales=act_scales[:, s * SOURCE_PASSES + g, :],
-                    in_=act_grouped[s][:, g * BATCH * PACK : (g + 1) * BATCH * PACK],
-                )
+        def regroup_activations(s, vector_tiles=()):
+            words = act_raw[s][:].bitcast(F32)
+            grouped_words = act_grouped[s][:].bitcast(F32).rearrange(
+                "q (g t r u) -> q g t r u", g=SOURCE_PASSES, t=BATCH_TILES, u=2
+            )
+            for t in range(BATCH_TILES):
+                regroup_rows(words[:, t, :], grouped_words[:, :, t], on_vector=(t in vector_tiles))
 
+        def quantise_activations(s):
+            columns = slice(s * SOURCE_PASSES * BATCH, (s + 1) * SOURCE_PASSES * BATCH)
+            nc.vector.quantize_mx(
+                out=act_codes[:, columns].bitcast(FP8X4), scales=act_scales[:, columns], in_=act_grouped[s][:]
+            )
+
+        w_sorted = {}
         w_grouped = {}
         w_codes = {}
         w_scales = {}
-        gate_rows = {}
-        gate_cols = {}
+
+        def sort_weights(ft, gate, sources, on_vector):
+            w_sorted[(ft, gate)] = work.tile([P, len(sources), FEATURES], BF16, name="w_sorted%d" % gate)
+            which = slice(sources[0], sources[-1] + 1)
+            out = w_sorted[(ft, gate)][:].bitcast(F32).rearrange("r s (g u q) -> r (s g) u q", g=SOURCE_PASSES, u=2)
+            raw = w_raw[gate][:].bitcast(F32)[:, ft, which].rearrange("r s (g q u) -> r (s g) u q", g=SOURCE_PASSES, u=2)
+            copy = nc.vector.tensor_copy if on_vector else nc.scalar.copy
+            copy(out=out, in_=raw)
 
         def transpose_weights(ft, gate, s, on_vector=False):
-            if s == 0:
-                w_grouped[(ft, gate)] = regrouped.tile([P, PASSES * P * PACK], BF16, name="w_grouped", align_bytes=64)
-            grouped_words = w_grouped[(ft, gate)][:].bitcast(F32).rearrange(
-                "q (s g r u) -> q s g r u", s=SOURCES, g=SOURCE_PASSES, u=2
+            if ft not in w_grouped:
+                w_grouped[ft] = weights.tile([P, GATES * PASSES * P * PACK], BF16, name="w_grouped", align_bytes=64)
+            grouped_words = w_grouped[ft][:].bitcast(F32).rearrange(
+                "q (z s g r u) -> q z s g r u", z=GATES, s=SOURCES, g=SOURCE_PASSES, u=2
             )
-            is_sorted = s in sorted_sources.get((ft, gate), ())
+            is_sorted = (ft, gate) in w_sorted and s < SORTED[gate]
             words = w_sorted[(ft, gate)][:, s] if is_sorted else w_raw[gate][:, ft, s]
-            regroup_rows(words.bitcast(F32), grouped_words[:, s], is_sorted, on_vector)
+            regroup_rows(words.bitcast(F32), grouped_words[:, gate, s], is_sorted, on_vector)
 
-        def quantise_weights(ft, gate):
-            codes = quantised.tile([P, PASSES * P], U32, name="w_codes", align_bytes=64)
-            scales = quantised.tile([P, PASSES * P], U8, name="w_scales", align_bytes=64)
-            nc.vector.quantize_mx(out=codes[:].bitcast(FP8X4), scales=scales[:], in_=w_grouped[(ft, gate)][:])
-            w_codes[(ft, gate)] = codes
-            w_scales[(ft, gate)] = scales
+        def quantise_weights(ft, first=0, last=GATES):
+            if first == 0:
+                w_codes[ft] = weights.tile([P, GATES * PASSES * P], U32, name="w_codes", align_bytes=64)
+                w_scales[ft] = weights.tile([P, GATES * PASSES * P], U8, name="w_scales", align_bytes=64)
+            columns = slice(first * PASSES * P, last * PASSES * P)
+            nc.vector.quantize_mx(
+                out=w_codes[ft][:, columns].bitcast(FP8X4),
+                scales=w_scales[ft][:, columns],
+                in_=w_grouped[ft][:, first * PASSES * P * PACK : last * PASSES * P * PACK],
+            )
 
         products = {}
+        gate_rows = {}
+        gate_cols = {}
+        input_terms = {}
 
         def multiply(ft, gate, first=0, last=BATCH_TILES):
             if first == 0:
                 products[(ft, gate)] = banks.tile([P, BATCH], F32, name="bank")
-            batch = slice(first * P, last * P)
             for k in range(PASSES):
-                columns = slice(k * P, (k + 1) * P)
+                columns = slice((gate * PASSES + k) * P, (gate * PASSES + k + 1) * P)
+                batch = slice(k * BATCH + first * P, k * BATCH + last * P)
                 nc.tensor.matmul_mx(
-                    out=products[(ft, gate)][:, batch],
-                    lhsT=w_codes[(ft, gate)][:, columns].bitcast(FP8X4),
-                    lhsT_scale=w_scales[(ft, gate)][:, columns],
-                    rhs=act_codes[:, k, batch].bitcast(FP8X4),
-                    rhs_scale=act_scales[:, k, batch],
+                    out=products[(ft, gate)][:, first * P : last * P],
+                    lhsT=w_codes[ft][:, columns].bitcast(FP8X4),
+                    lhsT_scale=w_scales[ft][:, columns],
+                    rhs=act_codes[:, batch].bitcast(FP8X4),
+                    rhs_scale=act_scales[:, batch],
                     start=(k == 0),
                     stop=(k == PASSES - 1),
                 )
@@ -214,122 +219,113 @@ def tile_slstmlayer_pb_kernel(
                 nc.tensor.transpose(bank[:, t, :], gate_rows[(ft, gate)][:, t * P : (t + 1) * P], identity[:])
             gate_cols[(ft, gate)] = bank
 
-        kept_terms = {}
-        input_terms = {}
+        def kept_product(first, last):
+            part = feature_columns(first, last)
+            nc.vector.tensor_tensor(out=cell[part], in0=f_sb[part], in1=c_sb[part], op=ALU.mult)
 
-        def kept_product(ft):
-            cols = slice(ft * P, (ft + 1) * P)
-            kept = work.tile([P, BATCH_TILES, P], F32, name="kept_term")
-            nc.vector.tensor_tensor(out=kept[:], in0=f_sb[:, :, cols], in1=c_sb[:, :, cols], op=ALU.mult)
-            kept_terms[ft] = kept
-
-        def reciprocal(ft):
-            cols = slice(ft * P, (ft + 1) * P)
-            nc.scalar.activation(out=norm[:, :, cols], in_=norm[:, :, cols], func=ACT.Square)
+        def reciprocal(first, last):
+            part = feature_columns(first, last)
+            nc.scalar.activation(out=norm[part], in_=norm[part], func=ACT.Square)
 
         def input_product(ft):
-            cols = slice(ft * P, (ft + 1) * P)
-            input_term = work.tile([P, BATCH_TILES, P], F32, name="input_term")
-            nc.vector.tensor_tensor(out=input_term[:], in0=gate_cols[(ft, 0)][:], in1=i_sb[:, :, cols], op=ALU.mult)
-            input_terms[ft] = input_term
+            pair, half = divmod(ft, 2)
+            if half == 0:
+                input_terms[pair] = work.tile([P, BATCH_TILES, 2 * P], F32, name="input_term")
+            out = input_terms[pair][:, :, half * P : (half + 1) * P]
+            nc.vector.tensor_tensor(out=out, in0=gate_cols[(ft, 0)][:], in1=i_sb[feature_columns(ft, ft + 1)], op=ALU.mult)
 
-        def finish_cell(ft):
-            cols = slice(ft * P, (ft + 1) * P)
-            nc.vector.tensor_tensor(out=cell[:, :, cols], in0=input_terms[ft][:], in1=kept_terms[ft][:], op=ALU.add)
-            nc.sync.dma_start(out=by_batch_tile(out_1)[:, :, cols], in_=cell[:, :, cols])
+        def finish_cell(first, last):
+            part = feature_columns(first, last)
+            pair, half = divmod(first, 2)
+            term = input_terms[pair][:, :, half * P : (half + last - first) * P]
+            nc.vector.tensor_tensor(out=cell[part], in0=cell[part], in1=term, op=ALU.add)
+            nc.sync.dma_start(out=by_batch_tile(out_1)[part], in_=cell[part])
 
         def output_product(ft, first=0, last=BATCH_TILES):
             part = (slice(None), slice(first, last), slice(ft * P, (ft + 1) * P))
             nc.vector.tensor_tensor(out=norm[part], in0=gate_cols[(ft, 1)][:, first:last, :], in1=norm[part], op=ALU.mult)
 
-        def finish_readout(ft, first=0, last=BATCH_TILES):
-            part = (slice(None), slice(first, last), slice(ft * P, (ft + 1) * P))
+        def finish_readout(ft, ft_last, first=0, last=BATCH_TILES):
+            part = (slice(None), slice(first, last), slice(ft * P, ft_last * P))
             nc.vector.tensor_tensor(out=norm[part], in0=norm[part], in1=cell[part], op=ALU.mult)
             nc.sync.dma_start(out=by_batch_tile(out_0)[part], in_=norm[part])
 
-        def regroup_activations(s, vector_tiles=()):
-            words = act_raw[s][:].bitcast(F32)
-            grouped_words = act_grouped[s][:].bitcast(F32).rearrange(
-                "q (g t r u) -> q g t r u", g=SOURCE_PASSES, t=BATCH_TILES, u=2
-            )
-            for t in range(BATCH_TILES):
-                regroup_rows(words[:, t, :], grouped_words[:, :, t], on_vector=(t in vector_tiles))
-
-        for step in (forget_products, normaliser_sum, clamp):
-            for t in (0, 1):
-                step(t)
-        regroup_activations(0)
+        forget_products(0, 1)
         bias_rows_f32 = keep.tile([P, P], F32, name="bias_rows_f32")
-        nc.vector.tensor_copy(out=bias_rows_f32[:], in_=bias_rows[:])
+        nc.gpsimd.tensor_copy(out=bias_rows_f32[:], in_=bias_rows[:])
+        forget_products(1, 2)
+        normaliser_sum(0, 2)
+        clamp(0, 2)
+        regroup_activations(0)
         bias_bank = banks.tile([P, BATCH_TILES, P], F32, name="bank")
         nc.tensor.transpose(bias_bank[:, 0, :], bias_rows_f32[:], identity[:])
         bias_cols = keep.tile([P, GATES * FEATURE_TILES], F32, name="bias_cols")
+        nc.scalar.copy(out=bias_cols[:], in_=bias_bank[:, 0, 0 : GATES * FEATURE_TILES])
         reciprocal_root(0)
         reciprocal_root(1)
         for s in range(SOURCES):
             for gate in range(GATES):
                 transpose_weights(0, gate, s)
         quantise_activations(0)
-        nc.vector.tensor_copy(out=bias_cols[:], in_=bias_bank[:, 0, 0 : GATES * FEATURE_TILES])
-        forget_products(2)
-        forget_products(3)
-        normaliser_sum(2)
-        for gate in range(GATES):
-            quantise_weights(0, gate)
-        normaliser_sum(3)
-        clamp(2)
-        clamp(3)
+        forget_products(2, 4)
+        normaliser_sum(2, 4)
+        quantise_weights(0)
+        clamp(2, 4)
         regroup_activations(1, ())
         reciprocal_root(2)
         reciprocal_root(3)
         nc.scalar.activation(out=warm[:], in_=ones[:], func=ACT.Sigmoid)
         quantise_activations(1)
 
-        def transposes(ft, gate):
-            ahead = ft + 1
-            behind = ft - 1
-            if ahead < FEATURE_TILES:
-                for s in range(SOURCES):
-                    transpose_weights(ahead, gate, s, on_vector=(ft == 0 and gate == 0))
-            if behind >= 0:
-                transpose_back(behind, gate)
-                if gate == 0:
-                    input_product(behind)
-                else:
-                    finish_cell(behind)
-                    output_product(behind)
-            if ahead < FEATURE_TILES:
-                quantise_weights(ahead, gate)
+        KEPT_TURNS = (1, 2)
 
         for ft in range(FEATURE_TILES):
+            ahead = ft + 1
+            behind = ft - 1
             if 1 <= ft < FEATURE_TILES - 2:
                 sort_weights(ft + 2, 0, (0,), on_vector=False)
-            if ft >= 1:
-                kept_product(ft - 1)
-            if ft >= 2:
-                finish_readout(ft - 2)
             for gate in range(GATES):
-                transposes(ft, gate)
+                if ahead < FEATURE_TILES:
+                    for s in range(SOURCES):
+                        transpose_weights(ahead, gate, s, on_vector=(ft == 0))
+                if behind >= 0:
+                    transpose_back(behind, gate)
+                    if gate == 0:
+                        input_product(behind)
+                if gate == 0 and ft in KEPT_TURNS:
+                    kept_product(4 * (ft - 1), 4 * ft)
+                if gate == 0 and ahead < FEATURE_TILES:
+                    quantise_weights(ahead, 0, 1)
                 if ft < FEATURE_TILES - 1 or gate == 0:
                     multiply(ft, gate)
                     activate(ft, gate)
+                if gate == 0:
+                    if ft in (2, 4, 6):
+                        finish_cell(ft - 2, ft)
+                    if ft in (3, 5, 7):
+                        finish_readout(ft - 3, ft - 1)
+                    if ft == 7:
+                        finish_cell(6, 7)
+            if ahead < FEATURE_TILES:
+                quantise_weights(ahead, 1, 2)
+            if behind >= 0:
+                output_product(behind)
             if ft == 0:
-                reciprocal(0)
-            if ft < FEATURE_TILES - 1:
-                reciprocal(ft + 1)
+                reciprocal(0, 1)
+            if ahead < FEATURE_TILES:
+                reciprocal(ahead, ahead + 1)
 
         last = FEATURE_TILES - 1
-        finish_readout(last - 1)
-        kept_product(last)
         multiply(last, 1, 0, 2)
         activate(last, 1, 0, 2)
         transpose_back(last, 0)
         input_product(last)
-        finish_cell(last)
+        finish_readout(last - 1, last)
+        finish_cell(last, last + 1)
         multiply(last, 1, 2, 4)
         activate(last, 1, 2, 4)
         transpose_back(last, 1)
         for half in (0, 2):
             output_product(last, half, half + 2)
         for half in (0, 2):
-            finish_readout(last, half, half + 2)
+            finish_readout(last, last + 1, half, half + 2)

@@ -185,10 +185,10 @@ def tile_slstmlayer_pb_kernel(
         gate_cols = {}
         input_terms = {}
 
-        def multiply(ft, gate, first=0, last=BATCH_TILES):
-            if first == 0:
+        def multiply(ft, gate, first=0, last=BATCH_TILES, passes=(0, PASSES)):
+            if first == 0 and passes[0] == 0:
                 products[(ft, gate)] = banks.tile([P, BATCH], F32, name="bank")
-            for k in range(PASSES):
+            for k in range(*passes):
                 columns = slice((gate * PASSES + k) * P, (gate * PASSES + k + 1) * P)
                 batch = slice(k * BATCH + first * P, k * BATCH + last * P)
                 nc.tensor.matmul_mx(
@@ -268,18 +268,32 @@ def tile_slstmlayer_pb_kernel(
                 transpose_weights(0, gate, s)
         quantise_activations(0)
         forget_products(2, 4)
-        normaliser_sum(2, 4)
+        normaliser_sum(2, 3)
+        normaliser_sum(3, 4)
+        clamp(2, 3)
+        clamp(3, 4)
         quantise_weights(0)
-        clamp(2, 4)
         regroup_activations(1, ())
         reciprocal_root(2)
         reciprocal_root(3)
         nc.scalar.activation(out=warm[:], in_=ones[:], func=ACT.Sigmoid)
         quantise_activations(1)
 
-        KEPT_TURNS = (1, 2)
-
-        for ft in range(FEATURE_TILES):
+        X_PASSES = (0, SOURCE_PASSES)
+        H_PASSES = (SOURCE_PASSES, PASSES)
+        for s in range(SOURCES):
+            transpose_weights(1, 0, s, on_vector=True)
+        for passes in (X_PASSES, H_PASSES):
+            for gate in range(GATES):
+                multiply(0, gate, passes=passes)
+        for gate in range(GATES):
+            activate(0, gate)
+        quantise_weights(1, 0, 1)
+        for s in range(SOURCES):
+            transpose_weights(1, 1, s, on_vector=True)
+        quantise_weights(1, 1, 2)
+        reciprocal(0, 2)
+        for ft in range(1, FEATURE_TILES):
             ahead = ft + 1
             behind = ft - 1
             if 1 <= ft < FEATURE_TILES - 2:
@@ -287,31 +301,32 @@ def tile_slstmlayer_pb_kernel(
             for gate in range(GATES):
                 if ahead < FEATURE_TILES:
                     for s in range(SOURCES):
-                        transpose_weights(ahead, gate, s, on_vector=(ft == 0))
+                        transpose_weights(ahead, gate, s)
                 if behind >= 0:
                     transpose_back(behind, gate)
                     if gate == 0:
                         input_product(behind)
-                if gate == 0 and ft in KEPT_TURNS:
-                    kept_product(4 * (ft - 1), 4 * ft)
-                if gate == 0 and ahead < FEATURE_TILES:
-                    quantise_weights(ahead, 0, 1)
-                if ft < FEATURE_TILES - 1 or gate == 0:
-                    multiply(ft, gate)
-                    activate(ft, gate)
+                if ahead < FEATURE_TILES:
+                    quantise_weights(ahead, gate, gate + 1)
                 if gate == 0:
+                    if ft == 1:
+                        kept_product(0, 4)
+                    if ft == 3:
+                        kept_product(4, 6)
+                    if ft == 4:
+                        kept_product(6, 8)
                     if ft in (2, 4, 6):
                         finish_cell(ft - 2, ft)
                     if ft in (3, 5, 7):
                         finish_readout(ft - 3, ft - 1)
                     if ft == 7:
                         finish_cell(6, 7)
-            if ahead < FEATURE_TILES:
-                quantise_weights(ahead, 1, 2)
-            if behind >= 0:
-                output_product(behind)
-            if ft == 0:
-                reciprocal(0, 1)
+                if gate == 1:
+                    output_product(behind)
+                if ft < FEATURE_TILES - 1 or gate == 0:
+                    multiply(ft, gate)
+                    activate(ft, gate)
+
             if ahead < FEATURE_TILES:
                 reciprocal(ahead, ahead + 1)
 

@@ -24,7 +24,7 @@ WORDS = FEATURES // 2
 WORD_BLOCKS = WORDS // P
 GATES = 2
 N_FLOOR = 1e-6
-SORTED = (1, 0)
+SORTED = (1, 1)
 
 FLOPS = 2 * BATCH * (SOURCES * FEATURES) * (GATES * FEATURES)
 
@@ -298,6 +298,7 @@ def tile_slstmlayer_pb_kernel(
             behind = ft - 1
             if 1 <= ft < FEATURE_TILES - 2:
                 sort_weights(ft + 2, 0, (0,), on_vector=False)
+                sort_weights(ft + 2, 1, (0,), on_vector=True)
             for gate in range(GATES):
                 if ahead < FEATURE_TILES:
                     for s in range(SOURCES):

from contextlib import ExitStack

import concourse.mybir as mybir
from concourse.masks import make_identity

F32 = mybir.dt.float32
BF16 = mybir.dt.bfloat16
U32 = mybir.dt.uint32
U8 = mybir.dt.uint8
FP8X4 = mybir.dt.float8_e4m3fn_x4
ACT = mybir.ActivationFunctionType
ALU = mybir.AluOpType

P = 128
PACK = 4
BATCH = 512
FEATURES = 1024
BATCH_TILES = BATCH // P
FEATURE_TILES = FEATURES // P
SOURCES = 2
SOURCE_PASSES = FEATURES // (P * PACK)
PASSES = SOURCES * SOURCE_PASSES
WORDS = FEATURES // 2
WORD_BLOCKS = WORDS // P
GATES = 2
N_FLOOR = 1e-6
SORTED = (1, 1)

FLOPS = 2 * BATCH * (SOURCES * FEATURES) * (GATES * FEATURES)


def tile_slstmlayer_pb_kernel(
    tc, x, h_prev, c_prev, n_prev, i_prime, f_prime, Wz_x, b_z, Wz_h, Wo_x, b_o, Wo_h, out_0, out_1
):
    nc = tc.nc
    gate_function = (ACT.Tanh, ACT.Sigmoid)

    def by_batch_tile(dram):
        return dram.rearrange("(p t) f -> p t f", t=BATCH_TILES)

    def feature_columns(first, last):
        return (slice(None), slice(None), slice(first * P, last * P))

    with ExitStack() as ctx:
        ctx.enter_context(tc.manual_schedule())
        keep = ctx.enter_context(tc.tile_pool(name="keep", bufs=1))
        weights = ctx.enter_context(tc.tile_pool(name="weights", bufs=2))
        work = ctx.enter_context(tc.tile_pool(name="work", bufs=2))
        rows_pool = ctx.enter_context(tc.tile_pool(name="rows_pool", bufs=2 * GATES))
        banks = ctx.enter_context(tc.psum_pool(name="banks", bufs=8))

        identity = keep.tile([P, P], F32, name="identity")
        act_raw = [keep.tile([P, BATCH_TILES, FEATURES], BF16, name="act_raw%d" % s) for s in range(SOURCES)]
        w_raw = [
            keep.tile([P, FEATURE_TILES, SOURCES, FEATURES], BF16, name="w_raw%d" % gate) for gate in range(GATES)
        ]
        f_sb = keep.tile([P, BATCH_TILES, FEATURES], BF16, name="f_sb")
        n_sb = keep.tile([P, BATCH_TILES, FEATURES], BF16, name="n_sb")
        i_sb = keep.tile([P, BATCH_TILES, FEATURES], BF16, name="i_sb")
        c_sb = keep.tile([P, BATCH_TILES, FEATURES], BF16, name="c_sb")
        cell = keep.tile([P, BATCH_TILES, FEATURES], F32, name="cell")
        norm = keep.tile([P, BATCH_TILES, FEATURES], F32, name="norm")
        act_grouped = [
            keep.tile([P, SOURCE_PASSES * BATCH * PACK], BF16, name="act_grouped%d" % s, align_bytes=64)
            for s in range(SOURCES)
        ]
        act_codes = keep.tile([P, PASSES * BATCH], U32, name="act_codes", align_bytes=64)
        act_scales = keep.tile([P, PASSES * BATCH], U8, name="act_scales", align_bytes=64)

        ones = keep.tile([P, 1], F32, name="ones")
        warm = keep.tile([P, 1], F32, name="warm")
        nc.vector.memset(ones[:], 1.0)
        nc.scalar.activation(out=warm[:], in_=ones[:], func=ACT.Abs_reciprocal_sqrt)
        make_identity(nc, identity[:])
        bias_rows = keep.tile([P, P], BF16, name="bias_rows")
        nc.gpsimd.memset(bias_rows[:], 0.0)

        def load_weights(ft, sources=(0, 1)):
            for s in sources:
                for gate, dram in enumerate(((Wz_x, Wo_x), (Wz_h, Wo_h))[s]):
                    nc.sync.dma_start(out=w_raw[gate][:, ft, s, :], in_=dram[ft * P : (ft + 1) * P, :])

        def load_rows(sbuf, dram, first, last):
            nc.sync.dma_start(out=sbuf[:, first:last, :], in_=by_batch_tile(dram)[:, first:last, :])

        load_rows(f_sb, f_prime, 0, 1)
        load_rows(n_sb, n_prev, 0, 1)
        for gate, bias in enumerate((b_z, b_o)):
            nc.sync.dma_start(
                out=bias_rows[gate * FEATURE_TILES : (gate + 1) * FEATURE_TILES, :],
                in_=bias.rearrange("(r c) -> r c", c=P),
            )
        load_rows(f_sb, f_prime, 1, 2)
        load_rows(n_sb, n_prev, 1, 2)
        load_rows(i_sb, i_prime, 0, 2)
        load_rows(act_raw[0], x, 0, 2)
        load_rows(act_raw[0], x, 2, 4)
        load_weights(0, (0,))
        load_rows(f_sb, f_prime, 2, 4)
        load_rows(n_sb, n_prev, 2, 4)
        load_weights(0, (1,))
        load_rows(i_sb, i_prime, 2, 4)
        load_rows(act_raw[1], h_prev, 0, 2)
        load_rows(act_raw[1], h_prev, 2, 4)
        load_weights(1)
        load_weights(2)
        load_rows(c_sb, c_prev, 0, 4)
        for ft in range(3, FEATURE_TILES):
            load_weights(ft)

        def regroup_rows(words, grouped_words, is_sorted=False, on_vector=False):
            bank = banks.tile([P, WORD_BLOCKS, P], F32, name="bank")
            for j in range(WORD_BLOCKS):
                g, u = divmod(j, 2)
                block = words[:, j * P : (j + 1) * P] if is_sorted else words[:, 2 * P * g + u : 2 * P * (g + 1) : 2]
                nc.tensor.transpose(bank[:, j, :], block, identity[:])
            copy = nc.vector.tensor_copy if on_vector else nc.scalar.copy
            copy(out=grouped_words, in_=bank[:].rearrange("q (g u) r -> q g r u", u=2))

        def forget_products(first, last):
            part = (slice(None), slice(first, last))
            nc.vector.tensor_tensor(out=norm[part], in0=f_sb[part], in1=n_sb[part], op=ALU.mult)

        def normaliser_sum(first, last):
            part = (slice(None), slice(first, last))
            nc.vector.tensor_tensor(out=norm[part], in0=norm[part], in1=i_sb[part], op=ALU.add)

        def clamp(first, last):
            part = (slice(None), slice(first, last))
            nc.vector.tensor_scalar_max(out=norm[part], in0=norm[part], scalar1=N_FLOOR)

        def reciprocal_root(t):
            nc.scalar.activation(out=norm[:, t, :], in_=norm[:, t, :], func=ACT.Abs_reciprocal_sqrt)

        def regroup_activations(s, vector_tiles=()):
            words = act_raw[s][:].bitcast(F32)
            grouped_words = act_grouped[s][:].bitcast(F32).rearrange(
                "q (g t r u) -> q g t r u", g=SOURCE_PASSES, t=BATCH_TILES, u=2
            )
            for t in range(BATCH_TILES):
                regroup_rows(words[:, t, :], grouped_words[:, :, t], on_vector=(t in vector_tiles))

        def quantise_activations(s):
            columns = slice(s * SOURCE_PASSES * BATCH, (s + 1) * SOURCE_PASSES * BATCH)
            nc.vector.quantize_mx(
                out=act_codes[:, columns].bitcast(FP8X4), scales=act_scales[:, columns], in_=act_grouped[s][:]
            )

        w_sorted = {}
        w_grouped = {}
        w_codes = {}
        w_scales = {}

        def sort_weights(ft, gate, sources, on_vector):
            w_sorted[(ft, gate)] = work.tile([P, len(sources), FEATURES], BF16, name="w_sorted%d" % gate)
            which = slice(sources[0], sources[-1] + 1)
            out = w_sorted[(ft, gate)][:].bitcast(F32).rearrange("r s (g u q) -> r (s g) u q", g=SOURCE_PASSES, u=2)
            raw = w_raw[gate][:].bitcast(F32)[:, ft, which].rearrange("r s (g q u) -> r (s g) u q", g=SOURCE_PASSES, u=2)
            copy = nc.vector.tensor_copy if on_vector else nc.scalar.copy
            copy(out=out, in_=raw)

        def transpose_weights(ft, gate, s, on_vector=False):
            if ft not in w_grouped:
                w_grouped[ft] = weights.tile([P, GATES * PASSES * P * PACK], BF16, name="w_grouped", align_bytes=64)
            grouped_words = w_grouped[ft][:].bitcast(F32).rearrange(
                "q (z s g r u) -> q z s g r u", z=GATES, s=SOURCES, g=SOURCE_PASSES, u=2
            )
            is_sorted = (ft, gate) in w_sorted and s < SORTED[gate]
            words = w_sorted[(ft, gate)][:, s] if is_sorted else w_raw[gate][:, ft, s]
            regroup_rows(words.bitcast(F32), grouped_words[:, gate, s], is_sorted, on_vector)

        def quantise_weights(ft, first=0, last=GATES):
            if first == 0:
                w_codes[ft] = weights.tile([P, GATES * PASSES * P], U32, name="w_codes", align_bytes=64)
                w_scales[ft] = weights.tile([P, GATES * PASSES * P], U8, name="w_scales", align_bytes=64)
            columns = slice(first * PASSES * P, last * PASSES * P)
            nc.vector.quantize_mx(
                out=w_codes[ft][:, columns].bitcast(FP8X4),
                scales=w_scales[ft][:, columns],
                in_=w_grouped[ft][:, first * PASSES * P * PACK : last * PASSES * P * PACK],
            )

        products = {}
        gate_rows = {}
        gate_cols = {}
        input_terms = {}

        def multiply(ft, gate, first=0, last=BATCH_TILES, passes=(0, PASSES)):
            if first == 0 and passes[0] == 0:
                products[(ft, gate)] = banks.tile([P, BATCH], F32, name="bank")
            for k in range(*passes):
                columns = slice((gate * PASSES + k) * P, (gate * PASSES + k + 1) * P)
                batch = slice(k * BATCH + first * P, k * BATCH + last * P)
                nc.tensor.matmul_mx(
                    out=products[(ft, gate)][:, first * P : last * P],
                    lhsT=w_codes[ft][:, columns].bitcast(FP8X4),
                    lhsT_scale=w_scales[ft][:, columns],
                    rhs=act_codes[:, batch].bitcast(FP8X4),
                    rhs_scale=act_scales[:, batch],
                    start=(k == 0),
                    stop=(k == PASSES - 1),
                )

        def activate(ft, gate, first=0, last=BATCH_TILES):
            if first == 0:
                gate_rows[(ft, gate)] = rows_pool.tile([P, BATCH], F32, name="gate_rows")
            batch = slice(first * P, last * P)
            column = gate * FEATURE_TILES + ft
            nc.scalar.activation(
                out=gate_rows[(ft, gate)][:, batch],
                in_=products[(ft, gate)][:, batch],
                func=gate_function[gate],
                bias=bias_cols[:, column : column + 1],
            )

        def transpose_back(ft, gate):
            bank = banks.tile([P, BATCH_TILES, P], F32, name="bank")
            for t in range(BATCH_TILES):
                nc.tensor.transpose(bank[:, t, :], gate_rows[(ft, gate)][:, t * P : (t + 1) * P], identity[:])
            gate_cols[(ft, gate)] = bank

        def kept_product(first, last):
            part = feature_columns(first, last)
            nc.vector.tensor_tensor(out=cell[part], in0=f_sb[part], in1=c_sb[part], op=ALU.mult)

        def reciprocal(first, last):
            part = feature_columns(first, last)
            nc.scalar.activation(out=norm[part], in_=norm[part], func=ACT.Square)

        def input_product(ft):
            pair, half = divmod(ft, 2)
            if half == 0:
                input_terms[pair] = work.tile([P, BATCH_TILES, 2 * P], F32, name="input_term")
            out = input_terms[pair][:, :, half * P : (half + 1) * P]
            nc.vector.tensor_tensor(out=out, in0=gate_cols[(ft, 0)][:], in1=i_sb[feature_columns(ft, ft + 1)], op=ALU.mult)

        def finish_cell(first, last):
            part = feature_columns(first, last)
            pair, half = divmod(first, 2)
            term = input_terms[pair][:, :, half * P : (half + last - first) * P]
            nc.vector.tensor_tensor(out=cell[part], in0=cell[part], in1=term, op=ALU.add)
            nc.sync.dma_start(out=by_batch_tile(out_1)[part], in_=cell[part])

        def output_product(ft, first=0, last=BATCH_TILES):
            part = (slice(None), slice(first, last), slice(ft * P, (ft + 1) * P))
            nc.vector.tensor_tensor(out=norm[part], in0=gate_cols[(ft, 1)][:, first:last, :], in1=norm[part], op=ALU.mult)

        def finish_readout(ft, ft_last, first=0, last=BATCH_TILES):
            part = (slice(None), slice(first, last), slice(ft * P, ft_last * P))
            nc.vector.tensor_tensor(out=norm[part], in0=norm[part], in1=cell[part], op=ALU.mult)
            nc.sync.dma_start(out=by_batch_tile(out_0)[part], in_=norm[part])

        forget_products(0, 1)
        bias_rows_f32 = keep.tile([P, P], F32, name="bias_rows_f32")
        nc.gpsimd.tensor_copy(out=bias_rows_f32[:], in_=bias_rows[:])
        forget_products(1, 2)
        normaliser_sum(0, 2)
        clamp(0, 2)
        regroup_activations(0)
        bias_bank = banks.tile([P, BATCH_TILES, P], F32, name="bank")
        nc.tensor.transpose(bias_bank[:, 0, :], bias_rows_f32[:], identity[:])
        bias_cols = keep.tile([P, GATES * FEATURE_TILES], F32, name="bias_cols")
        nc.scalar.copy(out=bias_cols[:], in_=bias_bank[:, 0, 0 : GATES * FEATURE_TILES])
        reciprocal_root(0)
        reciprocal_root(1)
        for s in range(SOURCES):
            for gate in range(GATES):
                transpose_weights(0, gate, s)
        quantise_activations(0)
        forget_products(2, 4)
        normaliser_sum(2, 3)
        normaliser_sum(3, 4)
        clamp(2, 3)
        clamp(3, 4)
        quantise_weights(0)
        regroup_activations(1, ())
        reciprocal_root(2)
        reciprocal_root(3)
        nc.scalar.activation(out=warm[:], in_=ones[:], func=ACT.Sigmoid)
        quantise_activations(1)

        X_PASSES = (0, SOURCE_PASSES)
        H_PASSES = (SOURCE_PASSES, PASSES)
        for s in range(SOURCES):
            transpose_weights(1, 0, s, on_vector=True)
        for passes in (X_PASSES, H_PASSES):
            for gate in range(GATES):
                multiply(0, gate, passes=passes)
        for gate in range(GATES):
            activate(0, gate)
        quantise_weights(1, 0, 1)
        for s in range(SOURCES):
            transpose_weights(1, 1, s, on_vector=True)
        quantise_weights(1, 1, 2)
        reciprocal(0, 2)
        for ft in range(1, FEATURE_TILES):
            ahead = ft + 1
            behind = ft - 1
            if 1 <= ft < FEATURE_TILES - 2:
                sort_weights(ft + 2, 0, (0,), on_vector=False)
                sort_weights(ft + 2, 1, (0,), on_vector=True)
            for gate in range(GATES):
                if ahead < FEATURE_TILES:
                    for s in range(SOURCES):
                        transpose_weights(ahead, gate, s)
                if behind >= 0:
                    transpose_back(behind, gate)
                    if gate == 0:
                        input_product(behind)
                if ahead < FEATURE_TILES:
                    quantise_weights(ahead, gate, gate + 1)
                if gate == 0:
                    if ft == 1:
                        kept_product(0, 4)
                    if ft == 3:
                        kept_product(4, 6)
                    if ft == 4:
                        kept_product(6, 8)
                    if ft in (2, 4, 6):
                        finish_cell(ft - 2, ft)
                    if ft in (3, 5, 7):
                        finish_readout(ft - 3, ft - 1)
                    if ft == 7:
                        finish_cell(6, 7)
                if gate == 1:
                    output_product(behind)
                if ft < FEATURE_TILES - 1 or gate == 0:
                    multiply(ft, gate)
                    activate(ft, gate)

            if ahead < FEATURE_TILES:
                reciprocal(ahead, ahead + 1)

        last = FEATURE_TILES - 1
        multiply(last, 1, 0, 2)
        activate(last, 1, 0, 2)
        transpose_back(last, 0)
        input_product(last)
        finish_readout(last - 1, last)
        finish_cell(last, last + 1)
        multiply(last, 1, 2, 4)
        activate(last, 1, 2, 4)
        transpose_back(last, 1)
        for half in (0, 2):
            output_product(last, half, half + 2)
        for half in (0, 2):
            finish_readout(last, last + 1, half, half + 2)
